import numpy as np
import ml_dtypes


def mxq(x, axis, fmt="e4m3"):
    dtype, down = {"e4m3": (ml_dtypes.float8_e4m3fn, 7), "e5m2": (ml_dtypes.float8_e5m2, 14)}[fmt]
    v = np.moveaxis(np.asarray(x, np.float32).astype(ml_dtypes.bfloat16).astype(np.float64), axis, -1)
    blocks = v.reshape(v.shape[:-1] + (-1, 32))
    amax = np.abs(blocks).max(-1, keepdims=True)
    byte = np.maximum(np.where(amax > 0, np.frexp(amax)[1] - 1 + 127, 0) - down, 1)
    scale = np.exp2(byte - 127.0)
    codes = (blocks / scale).astype(np.float32).astype(dtype).astype(np.float64)
    return np.moveaxis((codes * scale).reshape(v.shape), -1, axis)


WIDE = False


def mx_kscale(k):
    if not WIDE:
        return np.ones(k)
    levels = np.array([10, -10, 5, -5, 0])
    a = np.random.permutation(np.resize(levels, k // 512 * 4)).reshape(k // 512, 4)
    idx = np.arange(k)
    return np.exp2(a[idx // 512, idx % 128 // 32])


BF16 = ml_dtypes.bfloat16


def bf(x):
    return np.asarray(x, np.float32).astype(BF16)


def f64(x):
    return np.asarray(x).astype(np.float64)


E2M1 = np.array([0.0, 0.5, 1.0, 1.5, 2.0, 3.0, 4.0, 6.0, -0.0, -0.5, -1.0, -1.5, -2.0, -3.0, -4.0, -6.0])


def pack_weight(w, fmt):
    k, n = w.shape
    w = f64(bf(w)).reshape(k // 32, 32, n)
    amax = np.abs(w).max(1)
    if fmt == "e4m3":
        byte = np.frexp(amax)[1] - 1 + 127 - 7
    else:
        mant, ex = np.frexp(amax / 6.0)
        byte = np.where(mant > 0.5, ex, ex - 1) + 127
    byte = np.clip(np.where(amax > 0, byte, 1), 1, 254)
    scaled = (w * np.exp2(127.0 - byte)[:, None, :]).reshape(k, n).astype(np.float32)
    by_word = np.ascontiguousarray(scaled.reshape(k // 512, 128, 4, n).transpose(0, 1, 3, 2))
    if fmt == "e4m3":
        words = by_word.astype(ml_dtypes.float8_e4m3fn).view(np.uint8)
    else:
        c = by_word.astype(ml_dtypes.float4_e2m1fn).view(np.uint8) & 0xF
        words = c[..., 0::2] | (c[..., 1::2] << 4)
    return np.ascontiguousarray(words), np.ascontiguousarray(byte.astype(np.uint8).reshape(k // 512, 16, n))


def unpack_weight(words, scales, fmt):
    g, p, n, _ = words.shape
    if fmt == "e4m3":
        vals = np.ascontiguousarray(words).view(ml_dtypes.float8_e4m3fn).astype(np.float64)
    else:
        nib = np.empty((g, p, n, 4), np.uint8)
        nib[..., 0::2] = words & 0xF
        nib[..., 1::2] = words >> 4
        vals = E2M1[nib]
    vals = vals * np.repeat(np.exp2(scales.astype(np.float64) - 127.0), 8, axis=1)[..., None]
    return vals.transpose(0, 1, 3, 2).reshape(g * 512, n)


B, S, H, I = 2, 256, 1024, 3072
FMT = "e4m3"


def silu(v):
    return v / (1.0 + np.exp(-v))


def ternary(shape):
    return np.random.randint(-1, 2, shape).astype(np.float64)


def setup_inputs():
    s, t = mx_kscale(H), mx_kscale(I)
    x = np.random.standard_normal((B, S, H)) * s
    gate_w = ternary((I, H)) / s[None, :]
    up_w = ternary((I, H)) / s[None, :]
    down_w = ternary((H, I)) / t[None, :]
    gate_s = np.random.uniform(0.5, 2.5, I) / np.sqrt(H)
    up_s = np.random.uniform(0.5, 2.5, I) / np.sqrt(H) * t
    down_s = np.random.uniform(0.5, 2.5, H) / np.sqrt(I)
    gate_w_words, gate_w_scales = pack_weight(np.ascontiguousarray(gate_w.T), FMT)
    up_w_words, up_w_scales = pack_weight(np.ascontiguousarray(up_w.T), FMT)
    down_w_words, down_w_scales = pack_weight(np.ascontiguousarray(down_w.T), FMT)
    return {"x": bf(x), "gate_w_words": gate_w_words, "gate_w_scales": gate_w_scales,
            "up_w_words": up_w_words, "up_w_scales": up_w_scales,
            "down_w_words": down_w_words, "down_w_scales": down_w_scales,
            "gate_s": bf(gate_s), "up_s": bf(up_s), "down_s": bf(down_s)}


def reference(x, gate_w_words, gate_w_scales, up_w_words, up_w_scales, down_w_words, down_w_scales, gate_s, up_s, down_s):
    x = f64(x)
    b, s, h = x.shape
    xq = mxq(x.reshape(b * s, h), 1, "e4m3")
    g = (xq @ unpack_weight(gate_w_words, gate_w_scales, FMT)) * f64(gate_s)
    u = (xq @ unpack_weight(up_w_words, up_w_scales, FMT)) * f64(up_s)
    hdn = silu(g) * u
    out = (mxq(hdn, 1, "e4m3") @ unpack_weight(down_w_words, down_w_scales, FMT)) * f64(down_s)
    return out.reshape(b, s, -1)

@@ -1,0 +1,234 @@
+from contextlib import ExitStack
+
+import concourse.mybir as mybir
+from concourse.masks import make_identity
+
+BF16 = mybir.dt.bfloat16
+F32 = mybir.dt.float32
+I32 = mybir.dt.int32
+U32 = mybir.dt.uint32
+U8 = mybir.dt.uint8
+FP8X4 = mybir.dt.float8_e4m3fn_x4
+MULT = mybir.AluOpType.mult
+SILU = mybir.ActivationFunctionType.Silu
+
+P = 128
+PACK = 4
+K_PASS = P * PACK
+N_PASS = 512
+
+TOKENS = 512
+HIDDEN = 1024
+INNER = 3072
+TOKEN_TILES = TOKENS // P
+X_PASSES = HIDDEN // K_PASS
+BLOCKS = INNER // N_PASS
+OUT_HALVES = HIDDEN // N_PASS
+
+GATE_ROW = 0
+UP_ROW = BLOCKS
+DOWN_ROW = 2 * BLOCKS
+VECTOR_ROWS = 2 * BLOCKS + OUT_HALVES
+
+FLOPS = 2 * TOKENS * HIDDEN * INNER * 3
+
+
+def words_by_partition(words):
+    return words.rearrange("g p n t -> g p (n t)").bitcast(I32).rearrange("g p n -> p g n")
+
+
+def tile_cudaternaryexpertmodule_kernel(
+    tc,
+    x,
+    gate_w_words,
+    gate_w_scales,
+    up_w_words,
+    up_w_scales,
+    down_w_words,
+    down_w_scales,
+    gate_s,
+    up_s,
+    down_s,
+    out,
+):
+    nc = tc.nc
+    x_rows = x.flatten_outer_dims()
+    out_rows = out.flatten_outer_dims()
+
+    with ExitStack() as ctx:
+        keep = ctx.enter_context(tc.tile_pool(name="keep", bufs=1))
+        work = ctx.enter_context(tc.tile_pool(name="work", bufs=3))
+        psum_mm = ctx.enter_context(tc.psum_pool(name="psum_mm", bufs=6))
+        psum_tp = ctx.enter_context(tc.psum_pool(name="psum_tp", bufs=2))
+
+        ident_f32 = keep.tile([P, P], F32, name="ident_f32")
+        make_identity(nc, ident_f32[:])
+        ident_bf16 = keep.tile([P, P], BF16, name="ident_bf16")
+        make_identity(nc, ident_bf16[:])
+
+        vector_rows = keep.tile([P, N_PASS], BF16, name="vector_rows")
+        nc.vector.memset(vector_rows[:], 0.0)
+
+        first_planes = keep.tile([P, INNER], U8, name="first_planes", align_bytes=64)
+        nc.vector.memset(first_planes[:].bitcast(I32), 0)
+        down_planes = keep.tile([P, 2, HIDDEN], U8, name="down_planes", align_bytes=64)
+        nc.vector.memset(down_planes[:].rearrange("p b n -> p (b n)").bitcast(I32), 0)
+
+        nc.sync.dma_start(out=vector_rows[GATE_ROW : GATE_ROW + BLOCKS, :], in_=gate_s.rearrange("(r c) -> r c", c=N_PASS))
+        nc.sync.dma_start(out=vector_rows[UP_ROW : UP_ROW + BLOCKS, :], in_=up_s.rearrange("(r c) -> r c", c=N_PASS))
+        nc.sync.dma_start(out=vector_rows[DOWN_ROW : DOWN_ROW + OUT_HALVES, :], in_=down_s.rearrange("(r c) -> r c", c=N_PASS))
+
+        x_sb = keep.tile([P, TOKEN_TILES, HIDDEN], BF16, name="x_sb")
+        for i in range(TOKEN_TILES):
+            nc.sync.dma_start(out=x_sb[:, i, :], in_=x_rows[P * i : P * (i + 1), :])
+
+        for quadrant in range(4):
+            rows = slice(4 * quadrant, 4 * quadrant + 4)
+            nc.sync.dma_start(
+                out=first_planes[32 * quadrant : 32 * quadrant + 8, :].bitcast(I32),
+                in_=gate_w_scales[:, rows, :].bitcast(I32),
+            )
+            nc.sync.dma_start(
+                out=first_planes[32 * quadrant + 8 : 32 * quadrant + 16, :].bitcast(I32),
+                in_=up_w_scales[:, rows, :].bitcast(I32),
+            )
+
+        gate_words = keep.tile([P, X_PASSES, INNER], I32, name="gate_words", align_bytes=64)
+        up_words = keep.tile([P, X_PASSES, INNER], I32, name="up_words", align_bytes=64)
+        for c in range(BLOCKS):
+            cols = slice(N_PASS * c, N_PASS * (c + 1))
+            nc.sync.dma_start(out=gate_words[:, :, cols], in_=words_by_partition(gate_w_words)[:, :, cols])
+            nc.sync.dma_start(out=up_words[:, :, cols], in_=words_by_partition(up_w_words)[:, :, cols])
+
+        for quadrant in range(4):
+            rows = slice(4 * quadrant, 4 * quadrant + 4)
+            nc.sync.dma_start(
+                out=down_planes[32 * quadrant : 32 * quadrant + 16, 0, :].bitcast(I32),
+                in_=down_w_scales[0:4, rows, :].bitcast(I32),
+            )
+            nc.sync.dma_start(
+                out=down_planes[32 * quadrant : 32 * quadrant + 8, 1, :].bitcast(I32),
+                in_=down_w_scales[4:BLOCKS, rows, :].bitcast(I32),
+            )
+
+        down_words = keep.tile([P, BLOCKS, HIDDEN], I32, name="down_words", align_bytes=64)
+        for g in range(BLOCKS):
+            nc.sync.dma_start(out=down_words[:, g, :], in_=words_by_partition(down_w_words)[:, g, :])
+
+        spread = keep.tile([P, VECTOR_ROWS, N_PASS], BF16, name="spread")
+
+        def spread_row(row):
+            picked = psum_mm.tile([P, N_PASS], F32, tag="mm")
+            nc.tensor.matmul(
+                out=picked[:],
+                lhsT=ident_bf16[:, row : row + 1].to_broadcast([P, P]),
+                rhs=vector_rows[:],
+                start=True,
+                stop=True,
+            )
+            nc.scalar.copy(out=spread[:, row, :], in_=picked[:])
+
+        def quantise_pass(token_tiles, grouped, codes, scales):
+            grouped_words = grouped.bitcast(F32)
+            for pair in range(TOKEN_TILES // 2):
+                turned = psum_tp.tile([P, 2, 2 * P], F32, tag="tp")
+                for half in range(2):
+                    token_words = token_tiles[2 * pair + half].bitcast(F32)
+                    for u in range(2):
+                        nc.tensor.transpose(
+                            turned[:, u, P * half : P * (half + 1)],
+                            token_words[:, u : K_PASS // 2 : 2],
+                            ident_f32[:],
+                        )
+                nc.scalar.copy(
+                    out=grouped_words[:, 4 * P * pair : 4 * P * (pair + 1)].rearrange("p (w u) -> p w u", u=2),
+                    in_=turned[:].rearrange("p u w -> p w u"),
+                )
+            nc.vector.quantize_mx(out=codes.bitcast(FP8X4), scales=scales, in_=grouped)
+
+        x_grouped = keep.tile([P, X_PASSES, PACK * TOKENS], BF16, name="x_grouped", align_bytes=64)
+        x_codes = keep.tile([P, X_PASSES, TOKENS], U32, name="x_codes", align_bytes=64)
+        x_scales = keep.tile([P, X_PASSES, TOKENS], U8, name="x_scales", align_bytes=64)
+        for g in range(X_PASSES):
+            quantise_pass(
+                [x_sb[:, i, K_PASS * g : K_PASS * (g + 1)] for i in range(TOKEN_TILES)],
+                x_grouped[:, g, :],
+                x_codes[:, g, :],
+                x_scales[:, g, :],
+            )
+
+        h_codes = keep.tile([P, BLOCKS, TOKENS], U32, name="h_codes", align_bytes=64)
+        h_scales = keep.tile([P, BLOCKS, TOKENS], U8, name="h_scales", align_bytes=64)
+
+        def hidden_block(c, hidden):
+            cols = slice(N_PASS * c, N_PASS * (c + 1))
+            for i in range(TOKEN_TILES):
+                tokens = slice(P * i, P * (i + 1))
+                gate_ps = psum_mm.tile([P, N_PASS], F32, tag="mm")
+                up_ps = psum_mm.tile([P, N_PASS], F32, tag="mm")
+                for acc, words, first_row in ((gate_ps, gate_words, 0), (up_ps, up_words, 8)):
+                    for g in range(X_PASSES):
+                        nc.tensor.matmul_mx(
+                            out=acc[:],
+                            lhsT=x_codes[:, g, tokens].bitcast(FP8X4),
+                            lhsT_scale=x_scales[:, g, tokens],
+                            rhs=words[:, g, cols].bitcast(FP8X4),
+                            rhs_scale=first_planes[first_row + 4 * g : P, cols],
+                            start=(g == 0),
+                            stop=(g == X_PASSES - 1),
+                        )
+                gate = work.tile([P, N_PASS], F32, tag="gate")
+                nc.vector.tensor_tensor(out=gate[:], in0=gate_ps[:], in1=spread[:, GATE_ROW + c, :], op=MULT)
+                up = work.tile([P, N_PASS], F32, tag="up")
+                nc.vector.tensor_tensor(out=up[:], in0=up_ps[:], in1=spread[:, UP_ROW + c, :], op=MULT)
+                nc.scalar.activation(out=gate[:], in_=gate[:], func=SILU)
+                nc.gpsimd.tensor_tensor(out=hidden[:, i, :], in0=gate[:], in1=up[:], op=MULT)
+
+        def quantise_hidden(c, hidden):
+            h_grouped = work.tile([P, PACK * TOKENS], BF16, tag="h_grouped", bufs=2, align_bytes=64)
+            quantise_pass(
+                [hidden[:, i, :] for i in range(TOKEN_TILES)],
+                h_grouped[:],
+                h_codes[:, c, :],
+                h_scales[:, c, :],
+            )
+
+        spread_row(GATE_ROW)
+        spread_row(UP_ROW)
+        hidden_blocks = []
+        for c in range(BLOCKS):
+            if c + 1 < BLOCKS:
+                spread_row(GATE_ROW + c + 1)
+                spread_row(UP_ROW + c + 1)
+            hidden = work.tile([P, TOKEN_TILES, N_PASS], BF16, tag="hidden", bufs=2)
+            hidden_blocks.append(hidden)
+            hidden_block(c, hidden)
+            if c >= 1:
+                quantise_hidden(c - 1, hidden_blocks[c - 1])
+        quantise_hidden(BLOCKS - 1, hidden_blocks[BLOCKS - 1])
+        for half in range(OUT_HALVES):
+            spread_row(DOWN_ROW + half)
+
+        for pair in range(TOKEN_TILES // 2):
+            pieces = [(2 * pair + j, half) for j in range(2) for half in range(OUT_HALVES)]
+            accs = {}
+            for piece in pieces:
+                accs[piece] = psum_mm.tile([P, N_PASS], F32, tag="mm", name="out_ps")
+            for g in range(BLOCKS):
+                for i, half in pieces:
+                    tokens = slice(P * i, P * (i + 1))
+                    cols = slice(N_PASS * half, N_PASS * (half + 1))
+                    nc.tensor.matmul_mx(
+                        out=accs[(i, half)][:],
+                        lhsT=h_codes[:, g, tokens].bitcast(FP8X4),
+                        lhsT_scale=h_scales[:, g, tokens],
+                        rhs=down_words[:, g, cols].bitcast(FP8X4),
+                        rhs_scale=down_planes[4 * (g % 4) : P, g // 4, cols],
+                        start=(g == 0),
+                        stop=(g == BLOCKS - 1),
+                    )
+            for i, half in pieces:
+                cols = slice(N_PASS * half, N_PASS * (half + 1))
+                result = work.tile([P, N_PASS], F32, tag="result", bufs=4)
+                nc.vector.tensor_tensor(out=result[:], in0=accs[(i, half)][:], in1=spread[:, DOWN_ROW + half, :], op=MULT)
+                nc.sync.dma_start(out=out_rows[P * i : P * (i + 1), cols], in_=result[:])

@@ -25,8 +25,9 @@ X_PASSES = HIDDEN // K_PASS
 BLOCKS = INNER // N_PASS
 OUT_HALVES = HIDDEN // N_PASS
 
-GATE_ROW = 0
-UP_ROW = BLOCKS
+MM_BANKS = 6
+EARLY_TILES = MM_BANKS // OUT_HALVES
+
 DOWN_ROW = 2 * BLOCKS
 VECTOR_ROWS = 2 * BLOCKS + OUT_HALVES
 
@@ -56,15 +57,16 @@ def tile_cudaternaryexpertmodule_kernel(
     out_rows = out.flatten_outer_dims()
 
     with ExitStack() as ctx:
+        ctx.enter_context(tc.manual_schedule())
         keep = ctx.enter_context(tc.tile_pool(name="keep", bufs=1))
-        work = ctx.enter_context(tc.tile_pool(name="work", bufs=3))
-        psum_mm = ctx.enter_context(tc.psum_pool(name="psum_mm", bufs=6))
+        work = ctx.enter_context(tc.tile_pool(name="work", bufs=4))
+        psum_mm = ctx.enter_context(tc.psum_pool(name="psum_mm", bufs=MM_BANKS))
         psum_tp = ctx.enter_context(tc.psum_pool(name="psum_tp", bufs=2))
 
-        ident_f32 = keep.tile([P, P], F32, name="ident_f32")
-        make_identity(nc, ident_f32[:])
         ident_bf16 = keep.tile([P, P], BF16, name="ident_bf16")
         make_identity(nc, ident_bf16[:])
+        ident_f32 = keep.tile([P, P], F32, name="ident_f32")
+        make_identity(nc, ident_f32[:])
 
         vector_rows = keep.tile([P, N_PASS], BF16, name="vector_rows")
         nc.vector.memset(vector_rows[:], 0.0)
@@ -74,9 +76,9 @@ def tile_cudaternaryexpertmodule_kernel(
         down_planes = keep.tile([P, 2, HIDDEN], U8, name="down_planes", align_bytes=64)
         nc.vector.memset(down_planes[:].rearrange("p b n -> p (b n)").bitcast(I32), 0)
 
-        nc.sync.dma_start(out=vector_rows[GATE_ROW : GATE_ROW + BLOCKS, :], in_=gate_s.rearrange("(r c) -> r c", c=N_PASS))
-        nc.sync.dma_start(out=vector_rows[UP_ROW : UP_ROW + BLOCKS, :], in_=up_s.rearrange("(r c) -> r c", c=N_PASS))
-        nc.sync.dma_start(out=vector_rows[DOWN_ROW : DOWN_ROW + OUT_HALVES, :], in_=down_s.rearrange("(r c) -> r c", c=N_PASS))
+        nc.sync.dma_start(out=vector_rows[0:DOWN_ROW:2, :], in_=gate_s.rearrange("(r c) -> r c", c=N_PASS))
+        nc.sync.dma_start(out=vector_rows[1:DOWN_ROW:2, :], in_=up_s.rearrange("(r c) -> r c", c=N_PASS))
+        nc.sync.dma_start(out=vector_rows[DOWN_ROW:VECTOR_ROWS, :], in_=down_s.rearrange("(r c) -> r c", c=N_PASS))
 
         x_sb = keep.tile([P, TOKEN_TILES, HIDDEN], BF16, name="x_sb")
         for i in range(TOKEN_TILES):
@@ -117,48 +119,62 @@ def tile_cudaternaryexpertmodule_kernel(
 
         spread = keep.tile([P, VECTOR_ROWS, N_PASS], BF16, name="spread")
 
-        def spread_row(row):
-            picked = psum_mm.tile([P, N_PASS], F32, tag="mm")
-            nc.tensor.matmul(
-                out=picked[:],
-                lhsT=ident_bf16[:, row : row + 1].to_broadcast([P, P]),
-                rhs=vector_rows[:],
-                start=True,
-                stop=True,
-            )
-            nc.scalar.copy(out=spread[:, row, :], in_=picked[:])
+        def spread_two_rows(first_row):
+            picked = psum_mm.tile([P, 2, N_PASS], BF16, tag="mm")
+            for j in range(2):
+                row = first_row + j
+                nc.tensor.matmul(
+                    out=picked[:, j, :],
+                    lhsT=ident_bf16[:, row : row + 1].to_broadcast([P, P]),
+                    rhs=vector_rows[:],
+                    start=True,
+                    stop=True,
+                )
+            nc.scalar.copy(out=spread[:, first_row : first_row + 2, :], in_=picked[:])
 
-        def quantise_pass(token_tiles, grouped, codes, scales):
+        def turn(word_columns, grouped, copy_out):
             grouped_words = grouped.bitcast(F32)
             for pair in range(TOKEN_TILES // 2):
                 turned = psum_tp.tile([P, 2, 2 * P], F32, tag="tp")
                 for half in range(2):
-                    token_words = token_tiles[2 * pair + half].bitcast(F32)
                     for u in range(2):
                         nc.tensor.transpose(
                             turned[:, u, P * half : P * (half + 1)],
-                            token_words[:, u : K_PASS // 2 : 2],
+                            word_columns(2 * pair + half, u),
                             ident_f32[:],
                         )
-                nc.scalar.copy(
+                copy_out(
                     out=grouped_words[:, 4 * P * pair : 4 * P * (pair + 1)].rearrange("p (w u) -> p w u", u=2),
                     in_=turned[:].rearrange("p u w -> p w u"),
                 )
+
+        def quantise(grouped, codes, scales):
             nc.vector.quantize_mx(out=codes.bitcast(FP8X4), scales=scales, in_=grouped)
 
         x_grouped = keep.tile([P, X_PASSES, PACK * TOKENS], BF16, name="x_grouped", align_bytes=64)
         x_codes = keep.tile([P, X_PASSES, TOKENS], U32, name="x_codes", align_bytes=64)
         x_scales = keep.tile([P, X_PASSES, TOKENS], U8, name="x_scales", align_bytes=64)
+
+        spread_two_rows(0)
         for g in range(X_PASSES):
-            quantise_pass(
-                [x_sb[:, i, K_PASS * g : K_PASS * (g + 1)] for i in range(TOKEN_TILES)],
+            turn(
+                lambda i, u, g=g: x_sb[:, i, K_PASS * g : K_PASS * (g + 1)].bitcast(F32)[:, u : K_PASS // 2 : 2],
                 x_grouped[:, g, :],
-                x_codes[:, g, :],
-                x_scales[:, g, :],
+                nc.vector.tensor_copy,
             )
+        for g in range(X_PASSES):
+            quantise(x_grouped[:, g, :], x_codes[:, g, :], x_scales[:, g, :])
+        for first_row in range(2, VECTOR_ROWS, 2):
+            spread_two_rows(first_row)
 
         h_codes = keep.tile([P, BLOCKS, TOKENS], U32, name="h_codes", align_bytes=64)
         h_scales = keep.tile([P, BLOCKS, TOKENS], U8, name="h_scales", align_bytes=64)
+
+        def words_sorted(ap):
+            return ap.rearrange("t (p u e) -> t u p e", u=2, e=2)
+
+        def as_sorted(ap):
+            return ap.rearrange("t (u p e) -> t u p e", u=2, e=2)
 
         def hidden_block(c, hidden):
             cols = slice(N_PASS * c, N_PASS * (c + 1))
@@ -178,57 +194,78 @@ def tile_cudaternaryexpertmodule_kernel(
                             stop=(g == X_PASSES - 1),
                         )
                 gate = work.tile([P, N_PASS], F32, tag="gate")
-                nc.vector.tensor_tensor(out=gate[:], in0=gate_ps[:], in1=spread[:, GATE_ROW + c, :], op=MULT)
+                nc.vector.tensor_tensor(
+                    out=as_sorted(gate[:]),
+                    in0=words_sorted(gate_ps[:]),
+                    in1=words_sorted(spread[:, 2 * c, :]),
+                    op=MULT,
+                )
                 up = work.tile([P, N_PASS], F32, tag="up")
-                nc.vector.tensor_tensor(out=up[:], in0=up_ps[:], in1=spread[:, UP_ROW + c, :], op=MULT)
+                nc.vector.tensor_tensor(
+                    out=as_sorted(up[:]),
+                    in0=words_sorted(up_ps[:]),
+                    in1=words_sorted(spread[:, 2 * c + 1, :]),
+                    op=MULT,
+                )
                 nc.scalar.activation(out=gate[:], in_=gate[:], func=SILU)
                 nc.gpsimd.tensor_tensor(out=hidden[:, i, :], in0=gate[:], in1=up[:], op=MULT)
 
-        def quantise_hidden(c, hidden):
+        def turn_hidden(hidden):
             h_grouped = work.tile([P, PACK * TOKENS], BF16, tag="h_grouped", bufs=2, align_bytes=64)
-            quantise_pass(
-                [hidden[:, i, :] for i in range(TOKEN_TILES)],
+            turn(
+                lambda i, u: hidden[:, i, :].bitcast(F32)[:, P * u : P * (u + 1)],
                 h_grouped[:],
-                h_codes[:, c, :],
-                h_scales[:, c, :],
+                nc.scalar.copy,
             )
+            return h_grouped
 
-        spread_row(GATE_ROW)
-        spread_row(UP_ROW)
-        hidden_blocks = []
+        def quantise_hidden(c, h_grouped):
+            quantise(h_grouped[:], h_codes[:, c, :], h_scales[:, c, :])
+
+        hiddens = []
+        groupeds = []
         for c in range(BLOCKS):
-            if c + 1 < BLOCKS:
-                spread_row(GATE_ROW + c + 1)
-                spread_row(UP_ROW + c + 1)
             hidden = work.tile([P, TOKEN_TILES, N_PASS], BF16, tag="hidden", bufs=2)
-            hidden_blocks.append(hidden)
+            hiddens.append(hidden)
             hidden_block(c, hidden)
             if c >= 1:
-                quantise_hidden(c - 1, hidden_blocks[c - 1])
-        quantise_hidden(BLOCKS - 1, hidden_blocks[BLOCKS - 1])
-        for half in range(OUT_HALVES):
-            spread_row(DOWN_ROW + half)
+                groupeds.append(turn_hidden(hiddens[c - 1]))
+            if c >= 2:
+                quantise_hidden(c - 2, groupeds[c - 2])
+        quantise_hidden(BLOCKS - 2, groupeds[BLOCKS - 2])
 
-        for pair in range(TOKEN_TILES // 2):
-            pieces = [(2 * pair + j, half) for j in range(2) for half in range(OUT_HALVES)]
-            accs = {}
-            for piece in pieces:
-                accs[piece] = psum_mm.tile([P, N_PASS], F32, tag="mm", name="out_ps")
-            for g in range(BLOCKS):
-                for i, half in pieces:
-                    tokens = slice(P * i, P * (i + 1))
-                    cols = slice(N_PASS * half, N_PASS * (half + 1))
-                    nc.tensor.matmul_mx(
-                        out=accs[(i, half)][:],
-                        lhsT=h_codes[:, g, tokens].bitcast(FP8X4),
-                        lhsT_scale=h_scales[:, g, tokens],
-                        rhs=down_words[:, g, cols].bitcast(FP8X4),
-                        rhs_scale=down_planes[4 * (g % 4) : P, g // 4, cols],
-                        start=(g == 0),
-                        stop=(g == BLOCKS - 1),
-                    )
-            for i, half in pieces:
-                cols = slice(N_PASS * half, N_PASS * (half + 1))
-                result = work.tile([P, N_PASS], F32, tag="result", bufs=4)
-                nc.vector.tensor_tensor(out=result[:], in0=accs[(i, half)][:], in1=spread[:, DOWN_ROW + half, :], op=MULT)
-                nc.sync.dma_start(out=out_rows[P * i : P * (i + 1), cols], in_=result[:])
+        def down_pass(acc, i, half, g):
+            tokens = slice(P * i, P * (i + 1))
+            cols = slice(N_PASS * half, N_PASS * (half + 1))
+            nc.tensor.matmul_mx(
+                out=acc[:],
+                lhsT=h_codes[:, g, tokens].bitcast(FP8X4),
+                lhsT_scale=h_scales[:, g, tokens],
+                rhs=down_words[:, g, cols].bitcast(FP8X4),
+                rhs_scale=down_planes[4 * (g % 4) : P, g // 4, cols],
+                start=(g == 0),
+                stop=(g == BLOCKS - 1),
+            )
+
+        def finish(acc, i, half):
+            result = work.tile([P, N_PASS], F32, tag="result")
+            nc.vector.tensor_tensor(out=result[:], in0=acc[:], in1=spread[:, DOWN_ROW + half, :], op=MULT)
+            nc.sync.dma_start(out=out_rows[P * i : P * (i + 1), N_PASS * half : N_PASS * (half + 1)], in_=result[:])
+
+        early = [(i, half) for i in range(EARLY_TILES) for half in range(OUT_HALVES)]
+        accs = {}
+        for piece in early:
+            accs[piece] = psum_mm.tile([P, N_PASS], F32, tag="mm", name="out_ps")
+        for g in range(BLOCKS):
+            if g == BLOCKS - 2:
+                quantise_hidden(BLOCKS - 1, turn_hidden(hiddens[BLOCKS - 1]))
+            for i, half in early:
+                down_pass(accs[(i, half)], i, half, g)
+        for i, half in early:
+            finish(accs[(i, half)], i, half)
+        for i in range(EARLY_TILES, TOKEN_TILES):
+            for half in range(OUT_HALVES):
+                late_ps = psum_mm.tile([P, N_PASS], F32, tag="mm")
+                for g in range(BLOCKS):
+                    down_pass(late_ps, i, half, g)
+                finish(late_ps, i, half)

@@ -27,6 +27,7 @@ OUT_HALVES = HIDDEN // N_PASS
 
 MM_BANKS = 6
 EARLY_TILES = MM_BANKS // OUT_HALVES
+TILES_IN_FLIGHT = MM_BANKS // 2
 
 DOWN_ROW = 2 * BLOCKS
 VECTOR_ROWS = 2 * BLOCKS + OUT_HALVES
@@ -84,23 +85,27 @@ def tile_cudaternaryexpertmodule_kernel(
         for i in range(TOKEN_TILES):
             nc.sync.dma_start(out=x_sb[:, i, :], in_=x_rows[P * i : P * (i + 1), :])
 
-        for quadrant in range(4):
-            rows = slice(4 * quadrant, 4 * quadrant + 4)
-            nc.sync.dma_start(
-                out=first_planes[32 * quadrant : 32 * quadrant + 8, :].bitcast(I32),
-                in_=gate_w_scales[:, rows, :].bitcast(I32),
-            )
-            nc.sync.dma_start(
-                out=first_planes[32 * quadrant + 8 : 32 * quadrant + 16, :].bitcast(I32),
-                in_=up_w_scales[:, rows, :].bitcast(I32),
-            )
+        def load_first_planes(cols):
+            for quadrant in range(4):
+                rows = slice(4 * quadrant, 4 * quadrant + 4)
+                nc.sync.dma_start(
+                    out=first_planes[32 * quadrant : 32 * quadrant + 8, cols].bitcast(I32),
+                    in_=gate_w_scales[:, rows, cols].bitcast(I32),
+                )
+                nc.sync.dma_start(
+                    out=first_planes[32 * quadrant + 8 : 32 * quadrant + 16, cols].bitcast(I32),
+                    in_=up_w_scales[:, rows, cols].bitcast(I32),
+                )
 
         gate_words = keep.tile([P, X_PASSES, INNER], I32, name="gate_words", align_bytes=64)
         up_words = keep.tile([P, X_PASSES, INNER], I32, name="up_words", align_bytes=64)
+        load_first_planes(slice(0, N_PASS))
         for c in range(BLOCKS):
             cols = slice(N_PASS * c, N_PASS * (c + 1))
             nc.sync.dma_start(out=gate_words[:, :, cols], in_=words_by_partition(gate_w_words)[:, :, cols])
             nc.sync.dma_start(out=up_words[:, :, cols], in_=words_by_partition(up_w_words)[:, :, cols])
+            if c == 0:
+                load_first_planes(slice(N_PASS, INNER))
 
         for quadrant in range(4):
             rows = slice(4 * quadrant, 4 * quadrant + 4)
@@ -176,63 +181,63 @@ def tile_cudaternaryexpertmodule_kernel(
         def as_sorted(ap):
             return ap.rearrange("t (u p e) -> t u p e", u=2, e=2)
 
-        def hidden_block(c, hidden):
+        def hidden_tile(c, i, hidden):
             cols = slice(N_PASS * c, N_PASS * (c + 1))
-            for i in range(TOKEN_TILES):
-                tokens = slice(P * i, P * (i + 1))
-                gate_ps = psum_mm.tile([P, N_PASS], F32, tag="mm")
-                up_ps = psum_mm.tile([P, N_PASS], F32, tag="mm")
-                for acc, words, first_row in ((gate_ps, gate_words, 0), (up_ps, up_words, 8)):
-                    for g in range(X_PASSES):
-                        nc.tensor.matmul_mx(
-                            out=acc[:],
-                            lhsT=x_codes[:, g, tokens].bitcast(FP8X4),
-                            lhsT_scale=x_scales[:, g, tokens],
-                            rhs=words[:, g, cols].bitcast(FP8X4),
-                            rhs_scale=first_planes[first_row + 4 * g : P, cols],
-                            start=(g == 0),
-                            stop=(g == X_PASSES - 1),
-                        )
-                gate = work.tile([P, N_PASS], F32, tag="gate")
-                nc.vector.tensor_tensor(
-                    out=as_sorted(gate[:]),
-                    in0=words_sorted(gate_ps[:]),
-                    in1=words_sorted(spread[:, 2 * c, :]),
-                    op=MULT,
-                )
-                up = work.tile([P, N_PASS], F32, tag="up")
-                nc.vector.tensor_tensor(
-                    out=as_sorted(up[:]),
-                    in0=words_sorted(up_ps[:]),
-                    in1=words_sorted(spread[:, 2 * c + 1, :]),
-                    op=MULT,
-                )
-                nc.scalar.activation(out=gate[:], in_=gate[:], func=SILU)
-                nc.gpsimd.tensor_tensor(out=hidden[:, i, :], in0=gate[:], in1=up[:], op=MULT)
+            tokens = slice(P * i, P * (i + 1))
+            gate_ps = psum_mm.tile([P, N_PASS], F32, tag="mm")
+            up_ps = psum_mm.tile([P, N_PASS], F32, tag="mm")
+            for acc, words, first_row in ((gate_ps, gate_words, 0), (up_ps, up_words, 8)):
+                for g in range(X_PASSES):
+                    nc.tensor.matmul_mx(
+                        out=acc[:],
+                        lhsT=x_codes[:, g, tokens].bitcast(FP8X4),
+                        lhsT_scale=x_scales[:, g, tokens],
+                        rhs=words[:, g, cols].bitcast(FP8X4),
+                        rhs_scale=first_planes[first_row + 4 * g : P, cols],
+                        start=(g == 0),
+                        stop=(g == X_PASSES - 1),
+                    )
+            gate = work.tile([P, N_PASS], F32, tag="gate")
+            nc.vector.tensor_tensor(
+                out=as_sorted(gate[:]),
+                in0=words_sorted(gate_ps[:]),
+                in1=words_sorted(spread[:, 2 * c, :]),
+                op=MULT,
+            )
+            up = work.tile([P, N_PASS], F32, tag="up")
+            nc.vector.tensor_tensor(
+                out=as_sorted(up[:]),
+                in0=words_sorted(up_ps[:]),
+                in1=words_sorted(spread[:, 2 * c + 1, :]),
+                op=MULT,
+            )
+            nc.scalar.activation(out=gate[:], in_=gate[:], func=SILU)
+            nc.gpsimd.tensor_tensor(out=hidden[:, i, :], in0=gate[:], in1=up[:], op=MULT)
 
-        def turn_hidden(hidden):
-            h_grouped = work.tile([P, PACK * TOKENS], BF16, tag="h_grouped", bufs=2, align_bytes=64)
+        h_grouped = keep.tile([P, BLOCKS, PACK * TOKENS], BF16, name="h_grouped", align_bytes=64)
+
+        def turn_hidden(c, hidden):
             turn(
                 lambda i, u: hidden[:, i, :].bitcast(F32)[:, P * u : P * (u + 1)],
-                h_grouped[:],
+                h_grouped[:, c, :],
                 nc.scalar.copy,
             )
-            return h_grouped
 
-        def quantise_hidden(c, h_grouped):
-            quantise(h_grouped[:], h_codes[:, c, :], h_scales[:, c, :])
+        def quantise_hidden(c):
+            quantise(h_grouped[:, c, :], h_codes[:, c, :], h_scales[:, c, :])
 
         hiddens = []
-        groupeds = []
         for c in range(BLOCKS):
             hidden = work.tile([P, TOKEN_TILES, N_PASS], BF16, tag="hidden", bufs=2)
             hiddens.append(hidden)
-            hidden_block(c, hidden)
+            for i in range(TOKEN_TILES):
+                hidden_tile(c, i, hidden)
+                if c == BLOCKS - 1 and i == TOKEN_TILES - TILES_IN_FLIGHT:
+                    for turned_block in range(BLOCKS - 2):
+                        quantise_hidden(turned_block)
             if c >= 1:
-                groupeds.append(turn_hidden(hiddens[c - 1]))
-            if c >= 2:
-                quantise_hidden(c - 2, groupeds[c - 2])
-        quantise_hidden(BLOCKS - 2, groupeds[BLOCKS - 2])
+                turn_hidden(c - 1, hiddens[c - 1])
+        quantise_hidden(BLOCKS - 2)
 
         def down_pass(acc, i, half, g):
             tokens = slice(P * i, P * (i + 1))
@@ -254,11 +259,13 @@ def tile_cudaternaryexpertmodule_kernel(
 
         early = [(i, half) for i in range(EARLY_TILES) for half in range(OUT_HALVES)]
         accs = {}
-        for piece in early:
-            accs[piece] = psum_mm.tile([P, N_PASS], F32, tag="mm", name="out_ps")
-        for g in range(BLOCKS):
-            if g == BLOCKS - 2:
-                quantise_hidden(BLOCKS - 1, turn_hidden(hiddens[BLOCKS - 1]))
+        for i, half in early:
+            accs[(i, half)] = psum_mm.tile([P, N_PASS], F32, tag="mm", name="out_ps")
+            for g in range(BLOCKS - 2):
+                down_pass(accs[(i, half)], i, half, g)
+        turn_hidden(BLOCKS - 1, hiddens[BLOCKS - 1])
+        quantise_hidden(BLOCKS - 1)
+        for g in range(BLOCKS - 2, BLOCKS):
             for i, half in early:
                 down_pass(accs[(i, half)], i, half, g)
         for i, half in early:

@@ -212,7 +212,8 @@ def tile_cudaternaryexpertmodule_kernel(
                 op=MULT,
             )
             nc.scalar.activation(out=gate[:], in_=gate[:], func=SILU)
-            nc.gpsimd.tensor_tensor(out=hidden[:, i, :], in0=gate[:], in1=up[:], op=MULT)
+            product_engine = nc.vector if i == TOKEN_TILES - 1 else nc.gpsimd
+            product_engine.tensor_tensor(out=hidden[:, i, :], in0=gate[:], in1=up[:], op=MULT)
 
         h_grouped = keep.tile([P, BLOCKS, PACK * TOKENS], BF16, name="h_grouped", align_bytes=64)
 

@@ -28,6 +28,10 @@ OUT_HALVES = HIDDEN // N_PASS
 MM_BANKS = 6
 EARLY_TILES = MM_BANKS // OUT_HALVES
 TILES_IN_FLIGHT = MM_BANKS // 2
+AHEAD = 2
+
+GATE_PLANES = 0
+UP_PLANES = 8
 
 DOWN_ROW = 2 * BLOCKS
 VECTOR_ROWS = 2 * BLOCKS + OUT_HALVES
@@ -64,48 +68,51 @@ def tile_cudaternaryexpertmodule_kernel(
         psum_mm = ctx.enter_context(tc.psum_pool(name="psum_mm", bufs=MM_BANKS))
         psum_tp = ctx.enter_context(tc.psum_pool(name="psum_tp", bufs=2))
 
-        ident_bf16 = keep.tile([P, P], BF16, name="ident_bf16")
-        make_identity(nc, ident_bf16[:])
         ident_f32 = keep.tile([P, P], F32, name="ident_f32")
         make_identity(nc, ident_f32[:])
-
-        vector_rows = keep.tile([P, N_PASS], BF16, name="vector_rows")
-        nc.vector.memset(vector_rows[:], 0.0)
+        ident_bf16 = keep.tile([P, P], BF16, name="ident_bf16")
+        make_identity(nc, ident_bf16[:])
 
         first_planes = keep.tile([P, INNER], U8, name="first_planes", align_bytes=64)
         nc.vector.memset(first_planes[:].bitcast(I32), 0)
+        vector_rows = keep.tile([P, N_PASS], BF16, name="vector_rows")
+        nc.vector.memset(vector_rows[:], 0.0)
         down_planes = keep.tile([P, 2, HIDDEN], U8, name="down_planes", align_bytes=64)
         nc.vector.memset(down_planes[:].rearrange("p b n -> p (b n)").bitcast(I32), 0)
 
-        nc.sync.dma_start(out=vector_rows[0:DOWN_ROW:2, :], in_=gate_s.rearrange("(r c) -> r c", c=N_PASS))
-        nc.sync.dma_start(out=vector_rows[1:DOWN_ROW:2, :], in_=up_s.rearrange("(r c) -> r c", c=N_PASS))
-        nc.sync.dma_start(out=vector_rows[DOWN_ROW:VECTOR_ROWS, :], in_=down_s.rearrange("(r c) -> r c", c=N_PASS))
+        nc.gpsimd.dma_start(out=vector_rows[0:DOWN_ROW:2, :], in_=gate_s.rearrange("(r c) -> r c", c=N_PASS))
+        nc.gpsimd.dma_start(out=vector_rows[1:DOWN_ROW:2, :], in_=up_s.rearrange("(r c) -> r c", c=N_PASS))
+        nc.gpsimd.dma_start(out=vector_rows[DOWN_ROW:VECTOR_ROWS, :], in_=down_s.rearrange("(r c) -> r c", c=N_PASS))
 
         x_sb = keep.tile([P, TOKEN_TILES, HIDDEN], BF16, name="x_sb")
-        for i in range(TOKEN_TILES):
-            nc.sync.dma_start(out=x_sb[:, i, :], in_=x_rows[P * i : P * (i + 1), :])
+        for pair in range(TOKEN_TILES // 2):
+            tiles = slice(2 * pair, 2 * pair + 2)
+            nc.sync.dma_start(out=x_sb[:, tiles, :], in_=x_rows.rearrange("(i p) k -> p i k", p=P)[:, tiles, :])
 
-        def load_first_planes(cols):
+        def load_planes(scales, first_row, cols):
             for quadrant in range(4):
-                rows = slice(4 * quadrant, 4 * quadrant + 4)
+                top = 32 * quadrant + first_row
                 nc.sync.dma_start(
-                    out=first_planes[32 * quadrant : 32 * quadrant + 8, cols].bitcast(I32),
-                    in_=gate_w_scales[:, rows, cols].bitcast(I32),
-                )
-                nc.sync.dma_start(
-                    out=first_planes[32 * quadrant + 8 : 32 * quadrant + 16, cols].bitcast(I32),
-                    in_=up_w_scales[:, rows, cols].bitcast(I32),
+                    out=first_planes[top : top + 8, cols].bitcast(I32),
+                    in_=scales[:, 4 * quadrant : 4 * quadrant + 4, cols].bitcast(I32),
                 )
 
         gate_words = keep.tile([P, X_PASSES, INNER], I32, name="gate_words", align_bytes=64)
         up_words = keep.tile([P, X_PASSES, INNER], I32, name="up_words", align_bytes=64)
-        load_first_planes(slice(0, N_PASS))
-        for c in range(BLOCKS):
+
+        def load_words(c):
             cols = slice(N_PASS * c, N_PASS * (c + 1))
             nc.sync.dma_start(out=gate_words[:, :, cols], in_=words_by_partition(gate_w_words)[:, :, cols])
             nc.sync.dma_start(out=up_words[:, :, cols], in_=words_by_partition(up_w_words)[:, :, cols])
-            if c == 0:
-                load_first_planes(slice(N_PASS, INNER))
+
+        load_planes(gate_w_scales, GATE_PLANES, slice(0, AHEAD * N_PASS))
+        load_words(0)
+        load_planes(up_w_scales, UP_PLANES, slice(0, AHEAD * N_PASS))
+        for c in range(1, BLOCKS):
+            load_words(c)
+            if c == AHEAD - 1:
+                load_planes(gate_w_scales, GATE_PLANES, slice(AHEAD * N_PASS, INNER))
+                load_planes(up_w_scales, UP_PLANES, slice(AHEAD * N_PASS, INNER))
 
         for quadrant in range(4):
             rows = slice(4 * quadrant, 4 * quadrant + 4)
@@ -137,21 +144,19 @@ def tile_cudaternaryexpertmodule_kernel(
                 )
             nc.scalar.copy(out=spread[:, first_row : first_row + 2, :], in_=picked[:])
 
-        def turn(word_columns, grouped, copy_out):
-            grouped_words = grouped.bitcast(F32)
-            for pair in range(TOKEN_TILES // 2):
-                turned = psum_tp.tile([P, 2, 2 * P], F32, tag="tp")
-                for half in range(2):
-                    for u in range(2):
-                        nc.tensor.transpose(
-                            turned[:, u, P * half : P * (half + 1)],
-                            word_columns(2 * pair + half, u),
-                            ident_f32[:],
-                        )
-                copy_out(
-                    out=grouped_words[:, 4 * P * pair : 4 * P * (pair + 1)].rearrange("p (w u) -> p w u", u=2),
-                    in_=turned[:].rearrange("p u w -> p w u"),
-                )
+        def turn(word_columns, pair, grouped, copy_out):
+            turned = psum_tp.tile([P, 2, 2 * P], F32, tag="tp")
+            for half in range(2):
+                for u in range(2):
+                    nc.tensor.transpose(
+                        turned[:, u, P * half : P * (half + 1)],
+                        word_columns(2 * pair + half, u),
+                        ident_f32[:],
+                    )
+            copy_out(
+                out=grouped.bitcast(F32)[:, 4 * P * pair : 4 * P * (pair + 1)].rearrange("p (w u) -> p w u", u=2),
+                in_=turned[:].rearrange("p u w -> p w u"),
+            )
 
         def quantise(grouped, codes, scales):
             nc.vector.quantize_mx(out=codes.bitcast(FP8X4), scales=scales, in_=grouped)
@@ -160,17 +165,18 @@ def tile_cudaternaryexpertmodule_kernel(
         x_codes = keep.tile([P, X_PASSES, TOKENS], U32, name="x_codes", align_bytes=64)
         x_scales = keep.tile([P, X_PASSES, TOKENS], U8, name="x_scales", align_bytes=64)
 
-        spread_two_rows(0)
-        for g in range(X_PASSES):
-            turn(
-                lambda i, u, g=g: x_sb[:, i, K_PASS * g : K_PASS * (g + 1)].bitcast(F32)[:, u : K_PASS // 2 : 2],
-                x_grouped[:, g, :],
-                nc.vector.tensor_copy,
-            )
+        for pair in range(TOKEN_TILES // 2):
+            for g in range(X_PASSES):
+                turn(
+                    lambda i, u, g=g: x_sb[:, i, K_PASS * g : K_PASS * (g + 1)].bitcast(F32)[:, u : K_PASS // 2 : 2],
+                    pair,
+                    x_grouped[:, g, :],
+                    nc.vector.tensor_copy,
+                )
         for g in range(X_PASSES):
             quantise(x_grouped[:, g, :], x_codes[:, g, :], x_scales[:, g, :])
-        for first_row in range(2, VECTOR_ROWS, 2):
-            spread_two_rows(first_row)
+        for c in range(AHEAD):
+            spread_two_rows(2 * c)
 
         h_codes = keep.tile([P, BLOCKS, TOKENS], U32, name="h_codes", align_bytes=64)
         h_scales = keep.tile([P, BLOCKS, TOKENS], U8, name="h_scales", align_bytes=64)
@@ -186,7 +192,7 @@ def tile_cudaternaryexpertmodule_kernel(
             tokens = slice(P * i, P * (i + 1))
             gate_ps = psum_mm.tile([P, N_PASS], F32, tag="mm")
             up_ps = psum_mm.tile([P, N_PASS], F32, tag="mm")
-            for acc, words, first_row in ((gate_ps, gate_words, 0), (up_ps, up_words, 8)):
+            for acc, words, first_row in ((gate_ps, gate_words, GATE_PLANES), (up_ps, up_words, UP_PLANES)):
                 for g in range(X_PASSES):
                     nc.tensor.matmul_mx(
                         out=acc[:],
@@ -212,17 +218,18 @@ def tile_cudaternaryexpertmodule_kernel(
                 op=MULT,
             )
             nc.scalar.activation(out=gate[:], in_=gate[:], func=SILU)
-            product_engine = nc.vector if i == TOKEN_TILES - 1 else nc.gpsimd
-            product_engine.tensor_tensor(out=hidden[:, i, :], in0=gate[:], in1=up[:], op=MULT)
+            nc.gpsimd.tensor_tensor(out=hidden[:, i, :], in0=gate[:], in1=up[:], op=MULT)
 
         h_grouped = keep.tile([P, BLOCKS, PACK * TOKENS], BF16, name="h_grouped", align_bytes=64)
 
         def turn_hidden(c, hidden):
-            turn(
-                lambda i, u: hidden[:, i, :].bitcast(F32)[:, P * u : P * (u + 1)],
-                h_grouped[:, c, :],
-                nc.scalar.copy,
-            )
+            for pair in range(TOKEN_TILES // 2):
+                turn(
+                    lambda i, u: hidden[:, i, :].bitcast(F32)[:, P * u : P * (u + 1)],
+                    pair,
+                    h_grouped[:, c, :],
+                    nc.scalar.copy,
+                )
 
         def quantise_hidden(c):
             quantise(h_grouped[:, c, :], h_codes[:, c, :], h_scales[:, c, :])
@@ -236,6 +243,8 @@ def tile_cudaternaryexpertmodule_kernel(
                 if c == BLOCKS - 1 and i == TOKEN_TILES - TILES_IN_FLIGHT:
                     for turned_block in range(BLOCKS - 2):
                         quantise_hidden(turned_block)
+            if 2 * (c + AHEAD) < VECTOR_ROWS:
+                spread_two_rows(2 * (c + AHEAD))
             if c >= 1:
                 turn_hidden(c - 1, hiddens[c - 1])
         quantise_hidden(BLOCKS - 2)

@@ -62,7 +62,6 @@ def tile_cudaternaryexpertmodule_kernel(
     out_rows = out.flatten_outer_dims()
 
     with ExitStack() as ctx:
-        ctx.enter_context(tc.manual_schedule())
         keep = ctx.enter_context(tc.tile_pool(name="keep", bufs=1))
         work = ctx.enter_context(tc.tile_pool(name="work", bufs=4))
         psum_mm = ctx.enter_context(tc.psum_pool(name="psum_mm", bufs=MM_BANKS))

@@ -172,8 +172,13 @@ def tile_cudaternaryexpertmodule_kernel(
                     x_grouped[:, g, :],
                     nc.vector.tensor_copy,
                 )
-        for g in range(X_PASSES):
-            quantise(x_grouped[:, g, :], x_codes[:, g, :], x_scales[:, g, :])
+            tokens = slice(2 * P * pair, 2 * P * (pair + 1))
+            for g in range(X_PASSES):
+                quantise(
+                    x_grouped[:, g, PACK * 2 * P * pair : PACK * 2 * P * (pair + 1)],
+                    x_codes[:, g, tokens],
+                    x_scales[:, g, tokens],
+                )
         for c in range(AHEAD):
             spread_two_rows(2 * c)
 
@@ -186,7 +191,7 @@ def tile_cudaternaryexpertmodule_kernel(
         def as_sorted(ap):
             return ap.rearrange("t (u p e) -> t u p e", u=2, e=2)
 
-        def hidden_tile(c, i, hidden):
+        def gate_and_up(c, i):
             cols = slice(N_PASS * c, N_PASS * (c + 1))
             tokens = slice(P * i, P * (i + 1))
             gate_ps = psum_mm.tile([P, N_PASS], F32, tag="mm")
@@ -217,35 +222,42 @@ def tile_cudaternaryexpertmodule_kernel(
                 op=MULT,
             )
             nc.scalar.activation(out=gate[:], in_=gate[:], func=SILU)
-            nc.gpsimd.tensor_tensor(out=hidden[:, i, :], in0=gate[:], in1=up[:], op=MULT)
+            return gate, up
 
         h_grouped = keep.tile([P, BLOCKS, PACK * TOKENS], BF16, name="h_grouped", align_bytes=64)
 
-        def turn_hidden(c, hidden):
+        def turn_hidden(c, hidden, copies):
             for pair in range(TOKEN_TILES // 2):
                 turn(
                     lambda i, u: hidden[:, i, :].bitcast(F32)[:, P * u : P * (u + 1)],
                     pair,
                     h_grouped[:, c, :],
-                    nc.scalar.copy,
+                    copies[pair],
                 )
 
         def quantise_hidden(c):
             quantise(h_grouped[:, c, :], h_codes[:, c, :], h_scales[:, c, :])
 
         hiddens = []
+        left_to_vector = []
         for c in range(BLOCKS):
             hidden = work.tile([P, TOKEN_TILES, N_PASS], BF16, tag="hidden", bufs=2)
             hiddens.append(hidden)
             for i in range(TOKEN_TILES):
-                hidden_tile(c, i, hidden)
+                gate, up = gate_and_up(c, i)
+                if c == BLOCKS - 1 and i > TOKEN_TILES - TILES_IN_FLIGHT:
+                    left_to_vector.append((i, gate, up))
+                else:
+                    nc.gpsimd.tensor_tensor(out=hidden[:, i, :], in0=gate[:], in1=up[:], op=MULT)
                 if c == BLOCKS - 1 and i == TOKEN_TILES - TILES_IN_FLIGHT:
                     for turned_block in range(BLOCKS - 2):
                         quantise_hidden(turned_block)
             if 2 * (c + AHEAD) < VECTOR_ROWS:
                 spread_two_rows(2 * (c + AHEAD))
             if c >= 1:
-                turn_hidden(c - 1, hiddens[c - 1])
+                turn_hidden(c - 1, hiddens[c - 1], (nc.scalar.copy, nc.scalar.copy))
+        for i, gate, up in left_to_vector:
+            nc.vector.tensor_tensor(out=hiddens[BLOCKS - 1][:, i, :], in0=gate[:], in1=up[:], op=MULT)
         quantise_hidden(BLOCKS - 2)
 
         def down_pass(acc, i, half, g):
@@ -272,7 +284,7 @@ def tile_cudaternaryexpertmodule_kernel(
             accs[(i, half)] = psum_mm.tile([P, N_PASS], F32, tag="mm", name="out_ps")
             for g in range(BLOCKS - 2):
                 down_pass(accs[(i, half)], i, half, g)
-        turn_hidden(BLOCKS - 1, hiddens[BLOCKS - 1])
+        turn_hidden(BLOCKS - 1, hiddens[BLOCKS - 1], (nc.scalar.copy, nc.vector.tensor_copy))
         quantise_hidden(BLOCKS - 1)
         for g in range(BLOCKS - 2, BLOCKS):
             for i, half in early:

@@ -22,19 +22,17 @@ HIDDEN = 1024
 INNER = 3072
 TOKEN_TILES = TOKENS // P
 X_PASSES = HIDDEN // K_PASS
-BLOCKS = INNER // N_PASS
+BLOCKS = INNER // K_PASS
 OUT_HALVES = HIDDEN // N_PASS
 
-MM_BANKS = 6
-EARLY_TILES = MM_BANKS // OUT_HALVES
-TILES_IN_FLIGHT = MM_BANKS // 2
+BANKS = 8
+EARLY_TILES = 2
 AHEAD = 2
 
 GATE_PLANES = 0
 UP_PLANES = 8
 
-DOWN_ROW = 2 * BLOCKS
-VECTOR_ROWS = 2 * BLOCKS + OUT_HALVES
+VECTOR_PAD = 32
 
 FLOPS = 2 * TOKENS * HIDDEN * INNER * 3
 
@@ -63,25 +61,24 @@ def tile_cudaternaryexpertmodule_kernel(
 
     with ExitStack() as ctx:
         keep = ctx.enter_context(tc.tile_pool(name="keep", bufs=1))
-        work = ctx.enter_context(tc.tile_pool(name="work", bufs=4))
-        psum_mm = ctx.enter_context(tc.psum_pool(name="psum_mm", bufs=MM_BANKS))
-        psum_tp = ctx.enter_context(tc.psum_pool(name="psum_tp", bufs=2))
+        work = ctx.enter_context(tc.tile_pool(name="work", bufs=3))
+        psum = ctx.enter_context(tc.psum_pool(name="psum", bufs=BANKS))
 
-        ident_f32 = keep.tile([P, P], F32, name="ident_f32")
-        make_identity(nc, ident_f32[:])
-        ident_bf16 = keep.tile([P, P], BF16, name="ident_bf16")
-        make_identity(nc, ident_bf16[:])
-
-        first_planes = keep.tile([P, INNER], U8, name="first_planes", align_bytes=64)
-        nc.vector.memset(first_planes[:].bitcast(I32), 0)
-        vector_rows = keep.tile([P, N_PASS], BF16, name="vector_rows")
-        nc.vector.memset(vector_rows[:], 0.0)
+        loaded_planes = keep.tile([P, INNER], U8, name="loaded_planes", align_bytes=64)
+        nc.vector.memset(loaded_planes[:].bitcast(I32), 0)
         down_planes = keep.tile([P, 2, HIDDEN], U8, name="down_planes", align_bytes=64)
         nc.vector.memset(down_planes[:].rearrange("p b n -> p (b n)").bitcast(I32), 0)
+        ident_f32 = keep.tile([P, P], F32, name="ident_f32")
+        make_identity(nc, ident_f32[:])
+        table_warmer = keep.tile([P, 1], F32, name="table_warmer")
+        nc.scalar.activation(out=table_warmer[:], in_=ident_f32[:, 0:1], func=SILU)
 
-        nc.gpsimd.dma_start(out=vector_rows[0:DOWN_ROW:2, :], in_=gate_s.rearrange("(r c) -> r c", c=N_PASS))
-        nc.gpsimd.dma_start(out=vector_rows[1:DOWN_ROW:2, :], in_=up_s.rearrange("(r c) -> r c", c=N_PASS))
-        nc.gpsimd.dma_start(out=vector_rows[DOWN_ROW:VECTOR_ROWS, :], in_=down_s.rearrange("(r c) -> r c", c=N_PASS))
+        vector_cols_bf16 = keep.tile([P, 2, VECTOR_PAD], BF16, name="vector_cols_bf16")
+        for j, vector in enumerate((gate_s, up_s)):
+            nc.gpsimd.dma_start(
+                out=vector_cols_bf16[:, j, 0 : PACK * BLOCKS].rearrange("p (c t) -> p c t", t=PACK),
+                in_=vector.rearrange("(c p t) -> p c t", p=P, t=PACK),
+            )
 
         x_sb = keep.tile([P, TOKEN_TILES, HIDDEN], BF16, name="x_sb")
         for pair in range(TOKEN_TILES // 2):
@@ -92,26 +89,26 @@ def tile_cudaternaryexpertmodule_kernel(
             for quadrant in range(4):
                 top = 32 * quadrant + first_row
                 nc.sync.dma_start(
-                    out=first_planes[top : top + 8, cols].bitcast(I32),
+                    out=loaded_planes[top : top + 8, cols].bitcast(I32),
                     in_=scales[:, 4 * quadrant : 4 * quadrant + 4, cols].bitcast(I32),
                 )
 
-        gate_words = keep.tile([P, X_PASSES, INNER], I32, name="gate_words", align_bytes=64)
-        up_words = keep.tile([P, X_PASSES, INNER], I32, name="up_words", align_bytes=64)
+        gate_loaded = keep.tile([P, X_PASSES, INNER], I32, name="gate_loaded")
+        up_loaded = keep.tile([P, X_PASSES, INNER], I32, name="up_loaded")
 
         def load_words(c):
-            cols = slice(N_PASS * c, N_PASS * (c + 1))
-            nc.sync.dma_start(out=gate_words[:, :, cols], in_=words_by_partition(gate_w_words)[:, :, cols])
-            nc.sync.dma_start(out=up_words[:, :, cols], in_=words_by_partition(up_w_words)[:, :, cols])
+            cols = slice(K_PASS * c, K_PASS * (c + 1))
+            nc.sync.dma_start(out=gate_loaded[:, :, cols], in_=words_by_partition(gate_w_words)[:, :, cols])
+            nc.sync.dma_start(out=up_loaded[:, :, cols], in_=words_by_partition(up_w_words)[:, :, cols])
 
-        load_planes(gate_w_scales, GATE_PLANES, slice(0, AHEAD * N_PASS))
+        load_planes(gate_w_scales, GATE_PLANES, slice(0, AHEAD * K_PASS))
         load_words(0)
-        load_planes(up_w_scales, UP_PLANES, slice(0, AHEAD * N_PASS))
+        load_planes(up_w_scales, UP_PLANES, slice(0, AHEAD * K_PASS))
         for c in range(1, BLOCKS):
             load_words(c)
             if c == AHEAD - 1:
-                load_planes(gate_w_scales, GATE_PLANES, slice(AHEAD * N_PASS, INNER))
-                load_planes(up_w_scales, UP_PLANES, slice(AHEAD * N_PASS, INNER))
+                load_planes(gate_w_scales, GATE_PLANES, slice(AHEAD * K_PASS, INNER))
+                load_planes(up_w_scales, UP_PLANES, slice(AHEAD * K_PASS, INNER))
 
         for quadrant in range(4):
             rows = slice(4 * quadrant, 4 * quadrant + 4)
@@ -128,137 +125,104 @@ def tile_cudaternaryexpertmodule_kernel(
         for g in range(BLOCKS):
             nc.sync.dma_start(out=down_words[:, g, :], in_=words_by_partition(down_w_words)[:, g, :])
 
-        spread = keep.tile([P, VECTOR_ROWS, N_PASS], BF16, name="spread")
+        down_spread = keep.tile([P, HIDDEN], BF16, name="down_spread")
+        nc.sync.dma_start(out=down_spread[:], in_=down_s.partition_broadcast(P))
 
-        def spread_two_rows(first_row):
-            picked = psum_mm.tile([P, 2, N_PASS], BF16, tag="mm")
-            for j in range(2):
-                row = first_row + j
-                nc.tensor.matmul(
-                    out=picked[:, j, :],
-                    lhsT=ident_bf16[:, row : row + 1].to_broadcast([P, P]),
-                    rhs=vector_rows[:],
-                    start=True,
-                    stop=True,
-                )
-            nc.scalar.copy(out=spread[:, first_row : first_row + 2, :], in_=picked[:])
-
-        def turn(word_columns, pair, grouped, copy_out):
-            turned = psum_tp.tile([P, 2, 2 * P], F32, tag="tp")
-            for half in range(2):
-                for u in range(2):
-                    nc.tensor.transpose(
-                        turned[:, u, P * half : P * (half + 1)],
-                        word_columns(2 * pair + half, u),
-                        ident_f32[:],
-                    )
-            copy_out(
-                out=grouped.bitcast(F32)[:, 4 * P * pair : 4 * P * (pair + 1)].rearrange("p (w u) -> p w u", u=2),
-                in_=turned[:].rearrange("p u w -> p w u"),
-            )
-
-        def quantise(grouped, codes, scales):
-            nc.vector.quantize_mx(out=codes.bitcast(FP8X4), scales=scales, in_=grouped)
+        vector_cols = keep.tile([P, 2, PACK * BLOCKS], F32, name="vector_cols")
+        nc.vector.tensor_copy(out=vector_cols[:], in_=vector_cols_bf16[:, :, 0 : PACK * BLOCKS])
 
         x_grouped = keep.tile([P, X_PASSES, PACK * TOKENS], BF16, name="x_grouped", align_bytes=64)
         x_codes = keep.tile([P, X_PASSES, TOKENS], U32, name="x_codes", align_bytes=64)
         x_scales = keep.tile([P, X_PASSES, TOKENS], U8, name="x_scales", align_bytes=64)
 
+        def turn_x(pair, g, copy_out):
+            turned = psum.tile([P, 2, 2 * P], F32, tag="bank", name="turned")
+            for half in range(2):
+                words = x_sb[:, 2 * pair + half, K_PASS * g : K_PASS * (g + 1)].bitcast(F32)
+                for u in range(2):
+                    nc.tensor.transpose(
+                        turned[:, u, P * half : P * (half + 1)], words[:, u : K_PASS // 2 : 2], ident_f32[:]
+                    )
+            copy_out(
+                out=x_grouped[:, g, :].bitcast(F32)[:, 4 * P * pair : 4 * P * (pair + 1)].rearrange(
+                    "p (w u) -> p w u", u=2
+                ),
+                in_=turned[:].rearrange("p u w -> p w u"),
+            )
+
         for pair in range(TOKEN_TILES // 2):
-            for g in range(X_PASSES):
-                turn(
-                    lambda i, u, g=g: x_sb[:, i, K_PASS * g : K_PASS * (g + 1)].bitcast(F32)[:, u : K_PASS // 2 : 2],
-                    pair,
-                    x_grouped[:, g, :],
-                    nc.vector.tensor_copy,
-                )
+            turn_x(pair, 0, nc.vector.tensor_copy)
+            turn_x(pair, 1, nc.scalar.copy)
             tokens = slice(2 * P * pair, 2 * P * (pair + 1))
             for g in range(X_PASSES):
-                quantise(
-                    x_grouped[:, g, PACK * 2 * P * pair : PACK * 2 * P * (pair + 1)],
-                    x_codes[:, g, tokens],
-                    x_scales[:, g, tokens],
+                nc.vector.quantize_mx(
+                    out=x_codes[:, g, tokens].bitcast(FP8X4),
+                    scales=x_scales[:, g, tokens],
+                    in_=x_grouped[:, g, PACK * 2 * P * pair : PACK * 2 * P * (pair + 1)],
                 )
-        for c in range(AHEAD):
-            spread_two_rows(2 * c)
 
+        sorted_planes = keep.tile([P, INNER], U8, name="sorted_planes", align_bytes=64)
+        gate_sorted = keep.tile([P, X_PASSES, INNER], I32, name="gate_sorted", align_bytes=64)
+        up_sorted = keep.tile([P, X_PASSES, INNER], I32, name="up_sorted", align_bytes=64)
+
+        def sort_planes(c):
+            cols = slice(K_PASS * c, K_PASS * (c + 1))
+            nc.vector.tensor_copy(
+                out=sorted_planes[:, cols].rearrange("p (t m) -> p t m", t=PACK),
+                in_=loaded_planes[:, cols].rearrange("p (m t) -> p t m", t=PACK),
+            )
+
+        def sort_words(c, loaded, in_order):
+            cols = slice(K_PASS * c, K_PASS * (c + 1))
+            nc.vector.tensor_copy(
+                out=in_order[:, :, cols].rearrange("p g (t m) -> p g t m", t=PACK),
+                in_=loaded[:, :, cols].rearrange("p g (m t) -> p g t m", t=PACK),
+            )
+
+        for c in range(AHEAD):
+            sort_planes(c)
+            sort_words(c, gate_loaded, gate_sorted)
+            sort_words(c, up_loaded, up_sorted)
+
+        h_grouped = keep.tile([P, BLOCKS, PACK * TOKENS], BF16, name="h_grouped", align_bytes=64)
         h_codes = keep.tile([P, BLOCKS, TOKENS], U32, name="h_codes", align_bytes=64)
         h_scales = keep.tile([P, BLOCKS, TOKENS], U8, name="h_scales", align_bytes=64)
 
-        def words_sorted(ap):
-            return ap.rearrange("t (p u e) -> t u p e", u=2, e=2)
-
-        def as_sorted(ap):
-            return ap.rearrange("t (u p e) -> t u p e", u=2, e=2)
-
-        def gate_and_up(c, i):
-            cols = slice(N_PASS * c, N_PASS * (c + 1))
-            tokens = slice(P * i, P * (i + 1))
-            gate_ps = psum_mm.tile([P, N_PASS], F32, tag="mm")
-            up_ps = psum_mm.tile([P, N_PASS], F32, tag="mm")
-            for acc, words, first_row in ((gate_ps, gate_words, GATE_PLANES), (up_ps, up_words, UP_PLANES)):
+        def hidden_channels(c, t, hidden):
+            cols = slice(K_PASS * c + P * t, K_PASS * c + P * (t + 1))
+            gate_ps = psum.tile([P, TOKENS], F32, tag="bank", name="gate_ps")
+            up_ps = psum.tile([P, TOKENS], F32, tag="bank", name="up_ps")
+            for acc, words, first_row in ((gate_ps, gate_sorted, GATE_PLANES), (up_ps, up_sorted, UP_PLANES)):
                 for g in range(X_PASSES):
                     nc.tensor.matmul_mx(
                         out=acc[:],
-                        lhsT=x_codes[:, g, tokens].bitcast(FP8X4),
-                        lhsT_scale=x_scales[:, g, tokens],
-                        rhs=words[:, g, cols].bitcast(FP8X4),
-                        rhs_scale=first_planes[first_row + 4 * g : P, cols],
+                        lhsT=words[:, g, cols].bitcast(FP8X4),
+                        lhsT_scale=sorted_planes[first_row + 4 * g : P, cols],
+                        rhs=x_codes[:, g, :].bitcast(FP8X4),
+                        rhs_scale=x_scales[:, g, :],
                         start=(g == 0),
                         stop=(g == X_PASSES - 1),
                     )
-            gate = work.tile([P, N_PASS], F32, tag="gate")
-            nc.vector.tensor_tensor(
-                out=as_sorted(gate[:]),
-                in0=words_sorted(gate_ps[:]),
-                in1=words_sorted(spread[:, 2 * c, :]),
-                op=MULT,
+            col = PACK * c + t
+            gate = work.tile([P, TOKENS], F32, tag="gate")
+            nc.scalar.activation(out=gate[:], in_=gate_ps[:], func=SILU, scale=vector_cols[:, 0, col : col + 1])
+            nc.vector.scalar_tensor_tensor(
+                out=hidden[:, t, :],
+                in0=up_ps[:],
+                scalar=vector_cols[:, 1, col : col + 1],
+                in1=gate[:],
+                op0=MULT,
+                op1=MULT,
             )
-            up = work.tile([P, N_PASS], F32, tag="up")
-            nc.vector.tensor_tensor(
-                out=as_sorted(up[:]),
-                in0=words_sorted(up_ps[:]),
-                in1=words_sorted(spread[:, 2 * c + 1, :]),
-                op=MULT,
+
+        def group_hidden(c, hidden, i, copy):
+            copy(
+                out=h_grouped[:, c, PACK * P * i : PACK * P * (i + 1)].rearrange("p (n t) -> p n t", t=PACK),
+                in_=hidden[:, :, P * i : P * (i + 1)].rearrange("p t n -> p n t"),
             )
-            nc.scalar.activation(out=gate[:], in_=gate[:], func=SILU)
-            return gate, up
-
-        h_grouped = keep.tile([P, BLOCKS, PACK * TOKENS], BF16, name="h_grouped", align_bytes=64)
-
-        def turn_hidden(c, hidden, copies):
-            for pair in range(TOKEN_TILES // 2):
-                turn(
-                    lambda i, u: hidden[:, i, :].bitcast(F32)[:, P * u : P * (u + 1)],
-                    pair,
-                    h_grouped[:, c, :],
-                    copies[pair],
-                )
 
         def quantise_hidden(c):
-            quantise(h_grouped[:, c, :], h_codes[:, c, :], h_scales[:, c, :])
-
-        hiddens = []
-        left_to_vector = []
-        for c in range(BLOCKS):
-            hidden = work.tile([P, TOKEN_TILES, N_PASS], BF16, tag="hidden", bufs=2)
-            hiddens.append(hidden)
-            for i in range(TOKEN_TILES):
-                gate, up = gate_and_up(c, i)
-                if c == BLOCKS - 1 and i > TOKEN_TILES - TILES_IN_FLIGHT:
-                    left_to_vector.append((i, gate, up))
-                else:
-                    nc.gpsimd.tensor_tensor(out=hidden[:, i, :], in0=gate[:], in1=up[:], op=MULT)
-                if c == BLOCKS - 1 and i == TOKEN_TILES - TILES_IN_FLIGHT:
-                    for turned_block in range(BLOCKS - 2):
-                        quantise_hidden(turned_block)
-            if 2 * (c + AHEAD) < VECTOR_ROWS:
-                spread_two_rows(2 * (c + AHEAD))
-            if c >= 1:
-                turn_hidden(c - 1, hiddens[c - 1], (nc.scalar.copy, nc.scalar.copy))
-        for i, gate, up in left_to_vector:
-            nc.vector.tensor_tensor(out=hiddens[BLOCKS - 1][:, i, :], in0=gate[:], in1=up[:], op=MULT)
-        quantise_hidden(BLOCKS - 2)
+            nc.vector.quantize_mx(out=h_codes[:, c, :].bitcast(FP8X4), scales=h_scales[:, c, :], in_=h_grouped[:, c, :])
 
         def down_pass(acc, i, half, g):
             tokens = slice(P * i, P * (i + 1))
@@ -274,26 +238,59 @@ def tile_cudaternaryexpertmodule_kernel(
             )
 
         def finish(acc, i, half):
+            cols = slice(N_PASS * half, N_PASS * (half + 1))
             result = work.tile([P, N_PASS], F32, tag="result")
-            nc.vector.tensor_tensor(out=result[:], in0=acc[:], in1=spread[:, DOWN_ROW + half, :], op=MULT)
-            nc.sync.dma_start(out=out_rows[P * i : P * (i + 1), N_PASS * half : N_PASS * (half + 1)], in_=result[:])
+            nc.vector.tensor_tensor(out=result[:], in0=acc[:], in1=down_spread[:, cols], op=MULT)
+            nc.sync.dma_start(out=out_rows[P * i : P * (i + 1), cols], in_=result[:])
 
         early = [(i, half) for i in range(EARLY_TILES) for half in range(OUT_HALVES)]
         accs = {}
-        for i, half in early:
-            accs[(i, half)] = psum_mm.tile([P, N_PASS], F32, tag="mm", name="out_ps")
-            for g in range(BLOCKS - 2):
-                down_pass(accs[(i, half)], i, half, g)
-        turn_hidden(BLOCKS - 1, hiddens[BLOCKS - 1], (nc.scalar.copy, nc.vector.tensor_copy))
+
+        def early_pass(number):
+            g, which = divmod(number, len(early))
+            i, half = early[which]
+            if g == 0:
+                accs[(i, half)] = psum.tile([P, N_PASS], F32, tag="bank", name="out_ps")
+            down_pass(accs[(i, half)], i, half, g)
+
+        hiddens = []
+        passes_done = 0
+        for c in range(BLOCKS):
+            hiddens.append(work.tile([P, PACK, TOKENS], BF16, tag="hidden", name="hidden"))
+            for t in range(PACK):
+                hidden_channels(c, t, hiddens[c])
+                if c >= 1:
+                    group_hidden(c - 1, hiddens[c - 1], t, nc.scalar.copy)
+                if t == 0 and c >= 2:
+                    quantise_hidden(c - 2)
+                if c + AHEAD < BLOCKS:
+                    if t == 1:
+                        sort_words(c + AHEAD, gate_loaded, gate_sorted)
+                    if t == 2:
+                        sort_words(c + AHEAD, up_loaded, up_sorted)
+                    if t == 3:
+                        sort_planes(c + AHEAD)
+                if passes_done < len(early) * (c - 1) and (c, t) != (2, 0):
+                    early_pass(passes_done)
+                    passes_done += 1
+
+        quantise_hidden(BLOCKS - 2)
+        for i in range(TOKEN_TILES):
+            group_hidden(BLOCKS - 1, hiddens[BLOCKS - 1], i, nc.scalar.copy if i < 2 else nc.vector.tensor_copy)
+        for number in range(passes_done, len(early) * (BLOCKS - 1)):
+            early_pass(number)
+        for half in range(OUT_HALVES):
+            accs[(EARLY_TILES, half)] = psum.tile([P, N_PASS], F32, tag="bank", name="out_ps")
+            for g in range(BLOCKS - 1):
+                down_pass(accs[(EARLY_TILES, half)], EARLY_TILES, half, g)
         quantise_hidden(BLOCKS - 1)
-        for g in range(BLOCKS - 2, BLOCKS):
-            for i, half in early:
-                down_pass(accs[(i, half)], i, half, g)
-        for i, half in early:
-            finish(accs[(i, half)], i, half)
-        for i in range(EARLY_TILES, TOKEN_TILES):
+        for i in range(EARLY_TILES + 1):
             for half in range(OUT_HALVES):
-                late_ps = psum_mm.tile([P, N_PASS], F32, tag="mm")
+                down_pass(accs[(i, half)], i, half, BLOCKS - 1)
+                finish(accs[(i, half)], i, half)
+        for i in range(EARLY_TILES + 1, TOKEN_TILES):
+            for half in range(OUT_HALVES):
+                late_ps = psum.tile([P, N_PASS], F32, tag="bank", name="late_ps")
                 for g in range(BLOCKS):
                     down_pass(late_ps, i, half, g)
                 finish(late_ps, i, half)

@@ -26,8 +26,9 @@ BLOCKS = INNER // K_PASS
 OUT_HALVES = HIDDEN // N_PASS
 
 BANKS = 8
-EARLY_TILES = 2
-AHEAD = 2
+OUT_BANKS = TOKEN_TILES * OUT_HALVES
+FIRST_WAVE = 6
+PLANES_FIRST = 2
 
 GATE_PLANES = 0
 UP_PLANES = 8
@@ -63,6 +64,7 @@ def tile_cudaternaryexpertmodule_kernel(
         keep = ctx.enter_context(tc.tile_pool(name="keep", bufs=1))
         work = ctx.enter_context(tc.tile_pool(name="work", bufs=3))
         psum = ctx.enter_context(tc.psum_pool(name="psum", bufs=BANKS))
+        ctx.enter_context(tc.manual_schedule())
 
         loaded_planes = keep.tile([P, INNER], U8, name="loaded_planes", align_bytes=64)
         nc.vector.memset(loaded_planes[:].bitcast(I32), 0)
@@ -70,15 +72,16 @@ def tile_cudaternaryexpertmodule_kernel(
         nc.vector.memset(down_planes[:].rearrange("p b n -> p (b n)").bitcast(I32), 0)
         ident_f32 = keep.tile([P, P], F32, name="ident_f32")
         make_identity(nc, ident_f32[:])
-        table_warmer = keep.tile([P, 1], F32, name="table_warmer")
-        nc.scalar.activation(out=table_warmer[:], in_=ident_f32[:, 0:1], func=SILU)
 
         vector_cols_bf16 = keep.tile([P, 2, VECTOR_PAD], BF16, name="vector_cols_bf16")
         for j, vector in enumerate((gate_s, up_s)):
-            nc.gpsimd.dma_start(
+            nc.scalar.dma_start(
                 out=vector_cols_bf16[:, j, 0 : PACK * BLOCKS].rearrange("p (c t) -> p c t", t=PACK),
                 in_=vector.rearrange("(c p t) -> p c t", p=P, t=PACK),
             )
+
+        table_warmer = keep.tile([P, 1], F32, name="table_warmer")
+        nc.scalar.activation(out=table_warmer[:], in_=ident_f32[:, 0:1], func=SILU)
 
         x_sb = keep.tile([P, TOKEN_TILES, HIDDEN], BF16, name="x_sb")
         for pair in range(TOKEN_TILES // 2):
@@ -93,22 +96,23 @@ def tile_cudaternaryexpertmodule_kernel(
                     in_=scales[:, 4 * quadrant : 4 * quadrant + 4, cols].bitcast(I32),
                 )
 
-        gate_loaded = keep.tile([P, X_PASSES, INNER], I32, name="gate_loaded")
-        up_loaded = keep.tile([P, X_PASSES, INNER], I32, name="up_loaded")
+        gate_loaded = [keep.tile([P, X_PASSES, K_PASS], I32, name="gate_loaded%d" % c) for c in range(BLOCKS)]
+        up_loaded = [keep.tile([P, X_PASSES, K_PASS], I32, name="up_loaded%d" % c) for c in range(BLOCKS)]
 
-        def load_words(c):
+        def load_words(c, loaded, words):
             cols = slice(K_PASS * c, K_PASS * (c + 1))
-            nc.sync.dma_start(out=gate_loaded[:, :, cols], in_=words_by_partition(gate_w_words)[:, :, cols])
-            nc.sync.dma_start(out=up_loaded[:, :, cols], in_=words_by_partition(up_w_words)[:, :, cols])
+            nc.sync.dma_start(out=loaded[c][:], in_=words_by_partition(words)[:, :, cols])
 
-        load_planes(gate_w_scales, GATE_PLANES, slice(0, AHEAD * K_PASS))
-        load_words(0)
-        load_planes(up_w_scales, UP_PLANES, slice(0, AHEAD * K_PASS))
+        load_planes(gate_w_scales, GATE_PLANES, slice(0, PLANES_FIRST * K_PASS))
+        load_words(0, gate_loaded, gate_w_words)
+        load_planes(up_w_scales, UP_PLANES, slice(0, PLANES_FIRST * K_PASS))
+        load_words(0, up_loaded, up_w_words)
         for c in range(1, BLOCKS):
-            load_words(c)
-            if c == AHEAD - 1:
-                load_planes(gate_w_scales, GATE_PLANES, slice(AHEAD * K_PASS, INNER))
-                load_planes(up_w_scales, UP_PLANES, slice(AHEAD * K_PASS, INNER))
+            load_words(c, gate_loaded, gate_w_words)
+            load_words(c, up_loaded, up_w_words)
+            if c == PLANES_FIRST - 1:
+                load_planes(gate_w_scales, GATE_PLANES, slice(PLANES_FIRST * K_PASS, INNER))
+                load_planes(up_w_scales, UP_PLANES, slice(PLANES_FIRST * K_PASS, INNER))
 
         for quadrant in range(4):
             rows = slice(4 * quadrant, 4 * quadrant + 4)
@@ -150,20 +154,21 @@ def tile_cudaternaryexpertmodule_kernel(
                 in_=turned[:].rearrange("p u w -> p w u"),
             )
 
-        for pair in range(TOKEN_TILES // 2):
-            turn_x(pair, 0, nc.vector.tensor_copy)
-            turn_x(pair, 1, nc.scalar.copy)
+        def quantise_x(pair, g):
             tokens = slice(2 * P * pair, 2 * P * (pair + 1))
-            for g in range(X_PASSES):
-                nc.vector.quantize_mx(
-                    out=x_codes[:, g, tokens].bitcast(FP8X4),
-                    scales=x_scales[:, g, tokens],
-                    in_=x_grouped[:, g, PACK * 2 * P * pair : PACK * 2 * P * (pair + 1)],
-                )
+            nc.vector.quantize_mx(
+                out=x_codes[:, g, tokens].bitcast(FP8X4),
+                scales=x_scales[:, g, tokens],
+                in_=x_grouped[:, g, PACK * 2 * P * pair : PACK * 2 * P * (pair + 1)],
+            )
 
         sorted_planes = keep.tile([P, INNER], U8, name="sorted_planes", align_bytes=64)
-        gate_sorted = keep.tile([P, X_PASSES, INNER], I32, name="gate_sorted", align_bytes=64)
-        up_sorted = keep.tile([P, X_PASSES, INNER], I32, name="up_sorted", align_bytes=64)
+        gate_sorted = [
+            keep.tile([P, PACK, X_PASSES, P], I32, name="gate_sorted%d" % c, align_bytes=64) for c in range(BLOCKS)
+        ]
+        up_sorted = [
+            keep.tile([P, PACK, X_PASSES, P], I32, name="up_sorted%d" % c, align_bytes=64) for c in range(BLOCKS)
+        ]
 
         def sort_planes(c):
             cols = slice(K_PASS * c, K_PASS * (c + 1))
@@ -172,23 +177,42 @@ def tile_cudaternaryexpertmodule_kernel(
                 in_=loaded_planes[:, cols].rearrange("p (m t) -> p t m", t=PACK),
             )
 
-        def sort_words(c, loaded, in_order):
-            cols = slice(K_PASS * c, K_PASS * (c + 1))
+        def sort_words(c, loaded, in_order, ts):
             nc.vector.tensor_copy(
-                out=in_order[:, :, cols].rearrange("p g (t m) -> p g t m", t=PACK),
-                in_=loaded[:, :, cols].rearrange("p g (m t) -> p g t m", t=PACK),
+                out=in_order[c][:, ts, :, :],
+                in_=loaded[c][:].rearrange("p g (m t) -> p t g m", t=PACK)[:, ts, :, :],
             )
 
-        for c in range(AHEAD):
-            sort_planes(c)
-            sort_words(c, gate_loaded, gate_sorted)
-            sort_words(c, up_loaded, up_sorted)
+        for pair in range(TOKEN_TILES // 2):
+            for g in range(X_PASSES):
+                turn_x(pair, g, nc.scalar.copy)
+        quantise_x(0, 0)
+        quantise_x(0, 1)
+        quantise_x(1, 0)
+        sort_planes(0)
+        quantise_x(1, 1)
+        for t in range(PACK):
+            sort_words(0, gate_loaded, gate_sorted, slice(t, t + 1))
+            sort_words(0, up_loaded, up_sorted, slice(t, t + 1))
+        sort_jobs = []
+        for c in range(1, BLOCKS):
+            sort_jobs.append((c, None, None, None))
+            for loaded, in_order in ((gate_loaded, gate_sorted), (up_loaded, up_sorted)):
+                for first_t in range(0, PACK, 2):
+                    sort_jobs.append((c, loaded, in_order, slice(first_t, first_t + 2)))
+
+        def run_sort_job(job):
+            c, loaded, in_order, ts = job
+            if loaded is None:
+                sort_planes(c)
+            else:
+                sort_words(c, loaded, in_order, ts)
 
         h_grouped = keep.tile([P, BLOCKS, PACK * TOKENS], BF16, name="h_grouped", align_bytes=64)
         h_codes = keep.tile([P, BLOCKS, TOKENS], U32, name="h_codes", align_bytes=64)
         h_scales = keep.tile([P, BLOCKS, TOKENS], U8, name="h_scales", align_bytes=64)
 
-        def hidden_channels(c, t, hidden):
+        def multiply(c, t):
             cols = slice(K_PASS * c + P * t, K_PASS * c + P * (t + 1))
             gate_ps = psum.tile([P, TOKENS], F32, tag="bank", name="gate_ps")
             up_ps = psum.tile([P, TOKENS], F32, tag="bank", name="up_ps")
@@ -196,24 +220,14 @@ def tile_cudaternaryexpertmodule_kernel(
                 for g in range(X_PASSES):
                     nc.tensor.matmul_mx(
                         out=acc[:],
-                        lhsT=words[:, g, cols].bitcast(FP8X4),
+                        lhsT=words[c][:, t, g, :].bitcast(FP8X4),
                         lhsT_scale=sorted_planes[first_row + 4 * g : P, cols],
                         rhs=x_codes[:, g, :].bitcast(FP8X4),
                         rhs_scale=x_scales[:, g, :],
                         start=(g == 0),
                         stop=(g == X_PASSES - 1),
                     )
-            col = PACK * c + t
-            gate = work.tile([P, TOKENS], F32, tag="gate")
-            nc.scalar.activation(out=gate[:], in_=gate_ps[:], func=SILU, scale=vector_cols[:, 0, col : col + 1])
-            nc.vector.scalar_tensor_tensor(
-                out=hidden[:, t, :],
-                in0=up_ps[:],
-                scalar=vector_cols[:, 1, col : col + 1],
-                in1=gate[:],
-                op0=MULT,
-                op1=MULT,
-            )
+            return gate_ps, up_ps
 
         def group_hidden(c, hidden, i, copy):
             copy(
@@ -224,7 +238,34 @@ def tile_cudaternaryexpertmodule_kernel(
         def quantise_hidden(c):
             nc.vector.quantize_mx(out=h_codes[:, c, :].bitcast(FP8X4), scales=h_scales[:, c, :], in_=h_grouped[:, c, :])
 
-        def down_pass(acc, i, half, g):
+        hiddens = []
+        jobs_done = 0
+        for c in range(BLOCKS):
+            hiddens.append(work.tile([P, PACK, TOKENS], BF16, tag="hidden", name="hidden"))
+            for t in range(PACK):
+                gate_ps, up_ps = multiply(c, t)
+                col = PACK * c + t
+                gate = work.tile([P, TOKENS], F32, tag="gate", bufs=4)
+                nc.scalar.activation(out=gate[:], in_=gate_ps[:], func=SILU, scale=vector_cols[:, 0, col : col + 1])
+                if t == 0 and c >= 2:
+                    quantise_hidden(c - 2)
+                jobs_wanted = min(len(sort_jobs), (3 * (col + 1) + 1) // 2 + 1)
+                for job in sort_jobs[jobs_done:jobs_wanted]:
+                    run_sort_job(job)
+                jobs_done = jobs_wanted
+                nc.vector.scalar_tensor_tensor(
+                    out=hiddens[c][:, t, :],
+                    in0=up_ps[:],
+                    scalar=vector_cols[:, 1, col : col + 1],
+                    in1=gate[:],
+                    op0=MULT,
+                    op1=MULT,
+                )
+                if c >= 1:
+                    group_hidden(c - 1, hiddens[c - 1], t, nc.scalar.copy)
+
+        def down_pass(acc, a, g):
+            i, half = divmod(a, OUT_HALVES)
             tokens = slice(P * i, P * (i + 1))
             cols = slice(N_PASS * half, N_PASS * (half + 1))
             nc.tensor.matmul_mx(
@@ -237,60 +278,29 @@ def tile_cudaternaryexpertmodule_kernel(
                 stop=(g == BLOCKS - 1),
             )
 
-        def finish(acc, i, half):
+        def finish(acc, a):
+            i, half = divmod(a, OUT_HALVES)
             cols = slice(N_PASS * half, N_PASS * (half + 1))
             result = work.tile([P, N_PASS], F32, tag="result")
             nc.vector.tensor_tensor(out=result[:], in0=acc[:], in1=down_spread[:, cols], op=MULT)
             nc.sync.dma_start(out=out_rows[P * i : P * (i + 1), cols], in_=result[:])
 
-        early = [(i, half) for i in range(EARLY_TILES) for half in range(OUT_HALVES)]
-        accs = {}
-
-        def early_pass(number):
-            g, which = divmod(number, len(early))
-            i, half = early[which]
-            if g == 0:
-                accs[(i, half)] = psum.tile([P, N_PASS], F32, tag="bank", name="out_ps")
-            down_pass(accs[(i, half)], i, half, g)
-
-        hiddens = []
-        passes_done = 0
-        for c in range(BLOCKS):
-            hiddens.append(work.tile([P, PACK, TOKENS], BF16, tag="hidden", name="hidden"))
-            for t in range(PACK):
-                hidden_channels(c, t, hiddens[c])
-                if c >= 1:
-                    group_hidden(c - 1, hiddens[c - 1], t, nc.scalar.copy)
-                if t == 0 and c >= 2:
-                    quantise_hidden(c - 2)
-                if c + AHEAD < BLOCKS:
-                    if t == 1:
-                        sort_words(c + AHEAD, gate_loaded, gate_sorted)
-                    if t == 2:
-                        sort_words(c + AHEAD, up_loaded, up_sorted)
-                    if t == 3:
-                        sort_planes(c + AHEAD)
-                if passes_done < len(early) * (c - 1) and (c, t) != (2, 0):
-                    early_pass(passes_done)
-                    passes_done += 1
-
         quantise_hidden(BLOCKS - 2)
         for i in range(TOKEN_TILES):
             group_hidden(BLOCKS - 1, hiddens[BLOCKS - 1], i, nc.scalar.copy if i < 2 else nc.vector.tensor_copy)
-        for number in range(passes_done, len(early) * (BLOCKS - 1)):
-            early_pass(number)
-        for half in range(OUT_HALVES):
-            accs[(EARLY_TILES, half)] = psum.tile([P, N_PASS], F32, tag="bank", name="out_ps")
-            for g in range(BLOCKS - 1):
-                down_pass(accs[(EARLY_TILES, half)], EARLY_TILES, half, g)
+        accs = []
+        for a in range(FIRST_WAVE):
+            accs.append(psum.tile([P, N_PASS], F32, tag="bank", name="out_ps"))
+            for g in range(BLOCKS - 2):
+                down_pass(accs[a], a, g)
+        for a in range(FIRST_WAVE):
+            down_pass(accs[a], a, BLOCKS - 2)
         quantise_hidden(BLOCKS - 1)
-        for i in range(EARLY_TILES + 1):
-            for half in range(OUT_HALVES):
-                down_pass(accs[(i, half)], i, half, BLOCKS - 1)
-                finish(accs[(i, half)], i, half)
-        for i in range(EARLY_TILES + 1, TOKEN_TILES):
-            for half in range(OUT_HALVES):
-                late_ps = psum.tile([P, N_PASS], F32, tag="bank", name="late_ps")
-                for g in range(BLOCKS):
-                    down_pass(late_ps, i, half, g)
-                finish(late_ps, i, half)
+        for a in range(FIRST_WAVE):
+            down_pass(accs[a], a, BLOCKS - 1)
+            finish(accs[a], a)
+        for a in range(FIRST_WAVE, OUT_BANKS):
+            late_ps = psum.tile([P, N_PASS], F32, tag="bank", name="late_ps")
+            for g in range(BLOCKS):
+                down_pass(late_ps, a, g)
+            finish(late_ps, a)

@@ -281,7 +281,7 @@ def tile_cudaternaryexpertmodule_kernel(
         def finish(acc, a):
             i, half = divmod(a, OUT_HALVES)
             cols = slice(N_PASS * half, N_PASS * (half + 1))
-            result = work.tile([P, N_PASS], F32, tag="result")
+            result = work.tile([P, N_PASS], F32, tag="result", bufs=OUT_BANKS)
             nc.vector.tensor_tensor(out=result[:], in0=acc[:], in1=down_spread[:, cols], op=MULT)
             nc.sync.dma_start(out=out_rows[P * i : P * (i + 1), cols], in_=result[:])
 

@@ -164,23 +164,23 @@ def tile_cudaternaryexpertmodule_kernel(
 
         sorted_planes = keep.tile([P, INNER], U8, name="sorted_planes", align_bytes=64)
         gate_sorted = [
-            keep.tile([P, PACK, X_PASSES, P], I32, name="gate_sorted%d" % c, align_bytes=64) for c in range(BLOCKS)
+            keep.tile([P, X_PASSES, PACK, P], I32, name="gate_sorted%d" % c, align_bytes=64) for c in range(BLOCKS)
         ]
         up_sorted = [
-            keep.tile([P, PACK, X_PASSES, P], I32, name="up_sorted%d" % c, align_bytes=64) for c in range(BLOCKS)
+            keep.tile([P, X_PASSES, PACK, P], I32, name="up_sorted%d" % c, align_bytes=64) for c in range(BLOCKS)
         ]
 
         def sort_planes(c):
             cols = slice(K_PASS * c, K_PASS * (c + 1))
             nc.vector.tensor_copy(
-                out=sorted_planes[:, cols].rearrange("p (t m) -> p t m", t=PACK),
-                in_=loaded_planes[:, cols].rearrange("p (m t) -> p t m", t=PACK),
+                out=sorted_planes[:, cols].rearrange("p (t m) -> p m t", t=PACK),
+                in_=loaded_planes[:, cols].rearrange("p (m t) -> p m t", t=PACK),
             )
 
-        def sort_words(c, loaded, in_order, ts):
+        def sort_words(c, loaded, in_order, g):
             nc.vector.tensor_copy(
-                out=in_order[c][:, ts, :, :],
-                in_=loaded[c][:].rearrange("p g (m t) -> p t g m", t=PACK)[:, ts, :, :],
+                out=in_order[c][:, g, :, :].rearrange("p t m -> p m t"),
+                in_=loaded[c][:, g, :].rearrange("p (m t) -> p m t", t=PACK),
             )
 
         for pair in range(TOKEN_TILES // 2):
@@ -191,22 +191,24 @@ def tile_cudaternaryexpertmodule_kernel(
         quantise_x(1, 0)
         sort_planes(0)
         quantise_x(1, 1)
-        for t in range(PACK):
-            sort_words(0, gate_loaded, gate_sorted, slice(t, t + 1))
-            sort_words(0, up_loaded, up_sorted, slice(t, t + 1))
         sort_jobs = []
-        for c in range(1, BLOCKS):
-            sort_jobs.append((c, None, None, None))
+        for c in range(BLOCKS):
+            if c >= 1:
+                sort_jobs.append((c, None, None, None))
             for loaded, in_order in ((gate_loaded, gate_sorted), (up_loaded, up_sorted)):
-                for first_t in range(0, PACK, 2):
-                    sort_jobs.append((c, loaded, in_order, slice(first_t, first_t + 2)))
+                for g in range(X_PASSES):
+                    sort_jobs.append((c, loaded, in_order, g))
 
         def run_sort_job(job):
-            c, loaded, in_order, ts = job
+            c, loaded, in_order, g = job
             if loaded is None:
                 sort_planes(c)
             else:
-                sort_words(c, loaded, in_order, ts)
+                sort_words(c, loaded, in_order, g)
+
+        jobs_done = 2 * X_PASSES
+        for job in sort_jobs[0:jobs_done]:
+            run_sort_job(job)
 
         h_grouped = keep.tile([P, BLOCKS, PACK * TOKENS], BF16, name="h_grouped", align_bytes=64)
         h_codes = keep.tile([P, BLOCKS, TOKENS], U32, name="h_codes", align_bytes=64)
@@ -220,7 +222,7 @@ def tile_cudaternaryexpertmodule_kernel(
                 for g in range(X_PASSES):
                     nc.tensor.matmul_mx(
                         out=acc[:],
-                        lhsT=words[c][:, t, g, :].bitcast(FP8X4),
+                        lhsT=words[c][:, g, t, :].bitcast(FP8X4),
                         lhsT_scale=sorted_planes[first_row + 4 * g : P, cols],
                         rhs=x_codes[:, g, :].bitcast(FP8X4),
                         rhs_scale=x_scales[:, g, :],
@@ -239,7 +241,6 @@ def tile_cudaternaryexpertmodule_kernel(
             nc.vector.quantize_mx(out=h_codes[:, c, :].bitcast(FP8X4), scales=h_scales[:, c, :], in_=h_grouped[:, c, :])
 
         hiddens = []
-        jobs_done = 0
         for c in range(BLOCKS):
             hiddens.append(work.tile([P, PACK, TOKENS], BF16, tag="hidden", name="hidden"))
             for t in range(PACK):
@@ -249,7 +250,7 @@ def tile_cudaternaryexpertmodule_kernel(
                 nc.scalar.activation(out=gate[:], in_=gate_ps[:], func=SILU, scale=vector_cols[:, 0, col : col + 1])
                 if t == 0 and c >= 2:
                     quantise_hidden(c - 2)
-                jobs_wanted = min(len(sort_jobs), (3 * (col + 1) + 1) // 2 + 1)
+                jobs_wanted = min(len(sort_jobs), 2 * X_PASSES + (3 * (col + 1) + 1) // 2 + 1)
                 for job in sort_jobs[jobs_done:jobs_wanted]:
                     run_sort_job(job)
                 jobs_done = jobs_wanted

@@ -28,7 +28,10 @@ OUT_HALVES = HIDDEN // N_PASS
 BANKS = 8
 OUT_BANKS = TOKEN_TILES * OUT_HALVES
 FIRST_WAVE = 6
+LAST_PARTS = 2
 PLANES_FIRST = 2
+WARM_BEFORE_X = 6
+WARM_AFTER_X = 5
 
 GATE_PLANES = 0
 UP_PLANES = 8
@@ -70,8 +73,17 @@ def tile_cudaternaryexpertmodule_kernel(
         nc.vector.memset(loaded_planes[:].bitcast(I32), 0)
         down_planes = keep.tile([P, 2, HIDDEN], U8, name="down_planes", align_bytes=64)
         nc.vector.memset(down_planes[:].rearrange("p b n -> p (b n)").bitcast(I32), 0)
+        zeros = keep.tile([P, N_PASS], BF16, name="zeros")
+        nc.gpsimd.memset(zeros[:], 0.0)
         ident_f32 = keep.tile([P, P], F32, name="ident_f32")
         make_identity(nc, ident_f32[:])
+
+        def keep_warm(matmuls):
+            unused = psum.tile([P, N_PASS], F32, tag="bank", name="unused")
+            for n in range(matmuls):
+                nc.tensor.matmul(out=unused[:], lhsT=zeros[:, 0:P], rhs=zeros[:], start=True, stop=True)
+
+        keep_warm(WARM_BEFORE_X)
 
         vector_cols_bf16 = keep.tile([P, 2, VECTOR_PAD], BF16, name="vector_cols_bf16")
         for j, vector in enumerate((gate_s, up_s)):
@@ -186,6 +198,7 @@ def tile_cudaternaryexpertmodule_kernel(
         for pair in range(TOKEN_TILES // 2):
             for g in range(X_PASSES):
                 turn_x(pair, g, nc.scalar.copy)
+        keep_warm(WARM_AFTER_X)
         quantise_x(0, 0)
         quantise_x(0, 1)
         quantise_x(1, 0)
@@ -265,10 +278,11 @@ def tile_cudaternaryexpertmodule_kernel(
                 if c >= 1:
                     group_hidden(c - 1, hiddens[c - 1], t, nc.scalar.copy)
 
-        def down_pass(acc, a, g):
+        def down_pass(acc, a, g, part=0, parts=1):
             i, half = divmod(a, OUT_HALVES)
             tokens = slice(P * i, P * (i + 1))
-            cols = slice(N_PASS * half, N_PASS * (half + 1))
+            width = N_PASS // parts
+            cols = slice(N_PASS * half + width * part, N_PASS * half + width * (part + 1))
             nc.tensor.matmul_mx(
                 out=acc[:],
                 lhsT=h_codes[:, g, tokens].bitcast(FP8X4),
@@ -279,10 +293,11 @@ def tile_cudaternaryexpertmodule_kernel(
                 stop=(g == BLOCKS - 1),
             )
 
-        def finish(acc, a):
+        def finish(acc, a, part=0, parts=1):
             i, half = divmod(a, OUT_HALVES)
-            cols = slice(N_PASS * half, N_PASS * (half + 1))
-            result = work.tile([P, N_PASS], F32, tag="result", bufs=OUT_BANKS)
+            width = N_PASS // parts
+            cols = slice(N_PASS * half + width * part, N_PASS * half + width * (part + 1))
+            result = work.tile([P, width], F32, tag="result", bufs=OUT_BANKS + LAST_PARTS - 1)
             nc.vector.tensor_tensor(out=result[:], in0=acc[:], in1=down_spread[:, cols], op=MULT)
             nc.sync.dma_start(out=out_rows[P * i : P * (i + 1), cols], in_=result[:])
 
@@ -300,8 +315,13 @@ def tile_cudaternaryexpertmodule_kernel(
         for a in range(FIRST_WAVE):
             down_pass(accs[a], a, BLOCKS - 1)
             finish(accs[a], a)
-        for a in range(FIRST_WAVE, OUT_BANKS):
+        for a in range(FIRST_WAVE, OUT_BANKS - 1):
             late_ps = psum.tile([P, N_PASS], F32, tag="bank", name="late_ps")
             for g in range(BLOCKS):
                 down_pass(late_ps, a, g)
             finish(late_ps, a)
+        for part in range(LAST_PARTS):
+            part_ps = psum.tile([P, N_PASS // LAST_PARTS], F32, tag="bank", name="part_ps")
+            for g in range(BLOCKS):
+                down_pass(part_ps, OUT_BANKS - 1, g, part, LAST_PARTS)
+            finish(part_ps, OUT_BANKS - 1, part, LAST_PARTS)

@@ -85,16 +85,6 @@ def tile_cudaternaryexpertmodule_kernel(
 
         keep_warm(WARM_BEFORE_X)
 
-        vector_cols_bf16 = keep.tile([P, 2, VECTOR_PAD], BF16, name="vector_cols_bf16")
-        for j, vector in enumerate((gate_s, up_s)):
-            nc.scalar.dma_start(
-                out=vector_cols_bf16[:, j, 0 : PACK * BLOCKS].rearrange("p (c t) -> p c t", t=PACK),
-                in_=vector.rearrange("(c p t) -> p c t", p=P, t=PACK),
-            )
-
-        table_warmer = keep.tile([P, 1], F32, name="table_warmer")
-        nc.scalar.activation(out=table_warmer[:], in_=ident_f32[:, 0:1], func=SILU)
-
         x_sb = keep.tile([P, TOKEN_TILES, HIDDEN], BF16, name="x_sb")
         for pair in range(TOKEN_TILES // 2):
             tiles = slice(2 * pair, 2 * pair + 2)
@@ -117,35 +107,46 @@ def tile_cudaternaryexpertmodule_kernel(
 
         load_planes(gate_w_scales, GATE_PLANES, slice(0, PLANES_FIRST * K_PASS))
         load_words(0, gate_loaded, gate_w_words)
-        load_planes(up_w_scales, UP_PLANES, slice(0, PLANES_FIRST * K_PASS))
         load_words(0, up_loaded, up_w_words)
-        for c in range(1, BLOCKS):
-            load_words(c, gate_loaded, gate_w_words)
-            load_words(c, up_loaded, up_w_words)
-            if c == PLANES_FIRST - 1:
-                load_planes(gate_w_scales, GATE_PLANES, slice(PLANES_FIRST * K_PASS, INNER))
-                load_planes(up_w_scales, UP_PLANES, slice(PLANES_FIRST * K_PASS, INNER))
 
-        for quadrant in range(4):
-            rows = slice(4 * quadrant, 4 * quadrant + 4)
+        vector_cols_bf16 = keep.tile([P, 2, VECTOR_PAD], BF16, name="vector_cols_bf16")
+        for j, vector in enumerate((gate_s, up_s)):
             nc.sync.dma_start(
-                out=down_planes[32 * quadrant : 32 * quadrant + 16, 0, :].bitcast(I32),
-                in_=down_w_scales[0:4, rows, :].bitcast(I32),
+                out=vector_cols_bf16[:, j, 0 : PACK * BLOCKS].rearrange("p (c t) -> p c t", t=PACK),
+                in_=vector.rearrange("(c p t) -> p c t", p=P, t=PACK),
             )
-            nc.sync.dma_start(
-                out=down_planes[32 * quadrant : 32 * quadrant + 8, 1, :].bitcast(I32),
-                in_=down_w_scales[4:BLOCKS, rows, :].bitcast(I32),
-            )
+        vector_cols = keep.tile([P, 2, PACK * BLOCKS], F32, name="vector_cols")
+
+        def widen_vector(j):
+            nc.vector.tensor_copy(out=vector_cols[:, j, :], in_=vector_cols_bf16[:, j, 0 : PACK * BLOCKS])
+
+        table_warmer = keep.tile([P, 1], F32, name="table_warmer")
+        nc.scalar.activation(out=table_warmer[:], in_=ident_f32[:, 0:1], func=SILU)
 
         down_words = keep.tile([P, BLOCKS, HIDDEN], I32, name="down_words", align_bytes=64)
-        for g in range(BLOCKS):
-            nc.sync.dma_start(out=down_words[:, g, :], in_=words_by_partition(down_w_words)[:, g, :])
-
         down_spread = keep.tile([P, HIDDEN], BF16, name="down_spread")
-        nc.sync.dma_start(out=down_spread[:], in_=down_s.partition_broadcast(P))
 
-        vector_cols = keep.tile([P, 2, PACK * BLOCKS], F32, name="vector_cols")
-        nc.vector.tensor_copy(out=vector_cols[:], in_=vector_cols_bf16[:, :, 0 : PACK * BLOCKS])
+        def load_the_rest():
+            load_planes(up_w_scales, UP_PLANES, slice(0, PLANES_FIRST * K_PASS))
+            for c in range(1, BLOCKS):
+                load_words(c, gate_loaded, gate_w_words)
+                load_words(c, up_loaded, up_w_words)
+                if c == PLANES_FIRST - 1:
+                    load_planes(gate_w_scales, GATE_PLANES, slice(PLANES_FIRST * K_PASS, INNER))
+                    load_planes(up_w_scales, UP_PLANES, slice(PLANES_FIRST * K_PASS, INNER))
+            for quadrant in range(4):
+                rows = slice(4 * quadrant, 4 * quadrant + 4)
+                nc.sync.dma_start(
+                    out=down_planes[32 * quadrant : 32 * quadrant + 16, 0, :].bitcast(I32),
+                    in_=down_w_scales[0:4, rows, :].bitcast(I32),
+                )
+                nc.sync.dma_start(
+                    out=down_planes[32 * quadrant : 32 * quadrant + 8, 1, :].bitcast(I32),
+                    in_=down_w_scales[4:BLOCKS, rows, :].bitcast(I32),
+                )
+            for g in range(BLOCKS):
+                nc.sync.dma_start(out=down_words[:, g, :], in_=words_by_partition(down_w_words)[:, g, :])
+            nc.sync.dma_start(out=down_spread[:], in_=down_s.partition_broadcast(P))
 
         x_grouped = keep.tile([P, X_PASSES, PACK * TOKENS], BF16, name="x_grouped", align_bytes=64)
         x_codes = keep.tile([P, X_PASSES, TOKENS], U32, name="x_codes", align_bytes=64)
@@ -174,7 +175,8 @@ def tile_cudaternaryexpertmodule_kernel(
                 in_=x_grouped[:, g, PACK * 2 * P * pair : PACK * 2 * P * (pair + 1)],
             )
 
-        sorted_planes = keep.tile([P, INNER], U8, name="sorted_planes", align_bytes=64)
+        gate_planes = [keep.tile([P, K_PASS], U8, name="gate_planes%d" % c, align_bytes=64) for c in range(BLOCKS)]
+        up_planes = [keep.tile([P, K_PASS], U8, name="up_planes0", align_bytes=64)] + gate_planes[1:]
         gate_sorted = [
             keep.tile([P, X_PASSES, PACK, P], I32, name="gate_sorted%d" % c, align_bytes=64) for c in range(BLOCKS)
         ]
@@ -182,10 +184,10 @@ def tile_cudaternaryexpertmodule_kernel(
             keep.tile([P, X_PASSES, PACK, P], I32, name="up_sorted%d" % c, align_bytes=64) for c in range(BLOCKS)
         ]
 
-        def sort_planes(c):
+        def sort_planes(c, planes):
             cols = slice(K_PASS * c, K_PASS * (c + 1))
             nc.vector.tensor_copy(
-                out=sorted_planes[:, cols].rearrange("p (t m) -> p m t", t=PACK),
+                out=planes[c][:].rearrange("p (t m) -> p m t", t=PACK),
                 in_=loaded_planes[:, cols].rearrange("p (m t) -> p m t", t=PACK),
             )
 
@@ -201,13 +203,19 @@ def tile_cudaternaryexpertmodule_kernel(
         keep_warm(WARM_AFTER_X)
         quantise_x(0, 0)
         quantise_x(0, 1)
+        sort_planes(0, gate_planes)
+        load_the_rest()
         quantise_x(1, 0)
-        sort_planes(0)
         quantise_x(1, 1)
+        for loaded, in_order in ((gate_loaded, gate_sorted), (up_loaded, up_sorted)):
+            for g in range(X_PASSES):
+                sort_words(0, loaded, in_order, g)
+        sort_planes(0, up_planes)
+        widen_vector(0)
+        widen_vector(1)
         sort_jobs = []
-        for c in range(BLOCKS):
-            if c >= 1:
-                sort_jobs.append((c, None, None, None))
+        for c in range(1, BLOCKS):
+            sort_jobs.append((c, None, None, None))
             for loaded, in_order in ((gate_loaded, gate_sorted), (up_loaded, up_sorted)):
                 for g in range(X_PASSES):
                     sort_jobs.append((c, loaded, in_order, g))
@@ -215,34 +223,36 @@ def tile_cudaternaryexpertmodule_kernel(
         def run_sort_job(job):
             c, loaded, in_order, g = job
             if loaded is None:
-                sort_planes(c)
+                sort_planes(c, gate_planes)
             else:
                 sort_words(c, loaded, in_order, g)
 
-        jobs_done = 2 * X_PASSES
-        for job in sort_jobs[0:jobs_done]:
-            run_sort_job(job)
+        jobs_done = 0
 
         h_grouped = keep.tile([P, BLOCKS, PACK * TOKENS], BF16, name="h_grouped", align_bytes=64)
         h_codes = keep.tile([P, BLOCKS, TOKENS], U32, name="h_codes", align_bytes=64)
         h_scales = keep.tile([P, BLOCKS, TOKENS], U8, name="h_scales", align_bytes=64)
 
-        def multiply(c, t):
-            cols = slice(K_PASS * c + P * t, K_PASS * c + P * (t + 1))
-            gate_ps = psum.tile([P, TOKENS], F32, tag="bank", name="gate_ps")
-            up_ps = psum.tile([P, TOKENS], F32, tag="bank", name="up_ps")
-            for acc, words, first_row in ((gate_ps, gate_sorted, GATE_PLANES), (up_ps, up_sorted, UP_PLANES)):
-                for g in range(X_PASSES):
-                    nc.tensor.matmul_mx(
-                        out=acc[:],
-                        lhsT=words[c][:, g, t, :].bitcast(FP8X4),
-                        lhsT_scale=sorted_planes[first_row + 4 * g : P, cols],
-                        rhs=x_codes[:, g, :].bitcast(FP8X4),
-                        rhs_scale=x_scales[:, g, :],
-                        start=(g == 0),
-                        stop=(g == X_PASSES - 1),
-                    )
-            return gate_ps, up_ps
+        def multiply(c, t, words, planes, first_row):
+            acc = psum.tile([P, TOKENS], F32, tag="bank", name="acc")
+            for g in range(X_PASSES):
+                nc.tensor.matmul_mx(
+                    out=acc[:],
+                    lhsT=words[c][:, g, t, :].bitcast(FP8X4),
+                    lhsT_scale=planes[c][first_row + 4 * g : P, P * t : P * (t + 1)],
+                    rhs=x_codes[:, g, :].bitcast(FP8X4),
+                    rhs_scale=x_scales[:, g, :],
+                    start=(g == 0),
+                    stop=(g == X_PASSES - 1),
+                )
+            return acc
+
+        def silu_of_gate(c, t):
+            gate_ps = multiply(c, t, gate_sorted, gate_planes, GATE_PLANES)
+            gate = work.tile([P, TOKENS], F32, tag="gate", bufs=4)
+            col = PACK * c + t
+            nc.scalar.activation(out=gate[:], in_=gate_ps[:], func=SILU, scale=vector_cols[:, 0, col : col + 1])
+            return gate
 
         def group_hidden(c, hidden, i, copy):
             copy(
@@ -256,14 +266,14 @@ def tile_cudaternaryexpertmodule_kernel(
         hiddens = []
         for c in range(BLOCKS):
             hiddens.append(work.tile([P, PACK, TOKENS], BF16, tag="hidden", name="hidden"))
+            first_gates = [silu_of_gate(c, t) for t in range(PACK)] if c == 0 else None
             for t in range(PACK):
-                gate_ps, up_ps = multiply(c, t)
+                gate = first_gates[t] if c == 0 else silu_of_gate(c, t)
+                up_ps = multiply(c, t, up_sorted, up_planes, UP_PLANES)
                 col = PACK * c + t
-                gate = work.tile([P, TOKENS], F32, tag="gate", bufs=4)
-                nc.scalar.activation(out=gate[:], in_=gate_ps[:], func=SILU, scale=vector_cols[:, 0, col : col + 1])
                 if t == 0 and c >= 2:
                     quantise_hidden(c - 2)
-                jobs_wanted = min(len(sort_jobs), 2 * X_PASSES + (3 * (col + 1) + 1) // 2 + 1)
+                jobs_wanted = min(len(sort_jobs), (3 * (col + 1) + 1) // 2 + 1)
                 for job in sort_jobs[jobs_done:jobs_wanted]:
                     run_sort_job(job)
                 jobs_done = jobs_wanted

@@ -111,7 +111,7 @@ def tile_cudaternaryexpertmodule_kernel(
 
         vector_cols_bf16 = keep.tile([P, 2, VECTOR_PAD], BF16, name="vector_cols_bf16")
         for j, vector in enumerate((gate_s, up_s)):
-            nc.sync.dma_start(
+            nc.gpsimd.dma_start(
                 out=vector_cols_bf16[:, j, 0 : PACK * BLOCKS].rearrange("p (c t) -> p c t", t=PACK),
                 in_=vector.rearrange("(c p t) -> p c t", p=P, t=PACK),
             )

@@ -88,7 +88,12 @@ def tile_cudaternaryexpertmodule_kernel(
         x_sb = keep.tile([P, TOKEN_TILES, HIDDEN], BF16, name="x_sb")
         for pair in range(TOKEN_TILES // 2):
             tiles = slice(2 * pair, 2 * pair + 2)
-            nc.sync.dma_start(out=x_sb[:, tiles, :], in_=x_rows.rearrange("(i p) k -> p i k", p=P)[:, tiles, :])
+            nc.sync.dma_start(
+                out=x_sb[:, tiles, :].rearrange("p i k -> p (i k)"),
+                in_=x_rows.rearrange("(p i) k -> p (i k)", i=TOKEN_TILES)[
+                    :, 2 * HIDDEN * pair : 2 * HIDDEN * (pair + 1)
+                ],
+            )
 
         def load_planes(scales, first_row, cols):
             for quadrant in range(4):
@@ -126,26 +131,42 @@ def tile_cudaternaryexpertmodule_kernel(
         down_words = keep.tile([P, BLOCKS, HIDDEN], I32, name="down_words", align_bytes=64)
         down_spread = keep.tile([P, HIDDEN], BF16, name="down_spread")
 
+        def load_down_planes(group):
+            passes = slice(4 * group, min(4 * group + 4, BLOCKS))
+            for quadrant in range(4):
+                top = 32 * quadrant
+                nc.sync.dma_start(
+                    out=down_planes[top : top + 4 * (passes.stop - passes.start), group, :].bitcast(I32),
+                    in_=down_w_scales[passes, 4 * quadrant : 4 * quadrant + 4, :].bitcast(I32),
+                )
+
+        def load_down_words(g):
+            nc.sync.dma_start(out=down_words[:, g, :], in_=words_by_partition(down_w_words)[:, g, :])
+
         def load_the_rest():
             load_planes(up_w_scales, UP_PLANES, slice(0, PLANES_FIRST * K_PASS))
-            for c in range(1, BLOCKS):
-                load_words(c, gate_loaded, gate_w_words)
-                load_words(c, up_loaded, up_w_words)
-                if c == PLANES_FIRST - 1:
-                    load_planes(gate_w_scales, GATE_PLANES, slice(PLANES_FIRST * K_PASS, INNER))
-                    load_planes(up_w_scales, UP_PLANES, slice(PLANES_FIRST * K_PASS, INNER))
-            for quadrant in range(4):
-                rows = slice(4 * quadrant, 4 * quadrant + 4)
-                nc.sync.dma_start(
-                    out=down_planes[32 * quadrant : 32 * quadrant + 16, 0, :].bitcast(I32),
-                    in_=down_w_scales[0:4, rows, :].bitcast(I32),
-                )
-                nc.sync.dma_start(
-                    out=down_planes[32 * quadrant : 32 * quadrant + 8, 1, :].bitcast(I32),
-                    in_=down_w_scales[4:BLOCKS, rows, :].bitcast(I32),
-                )
-            for g in range(BLOCKS):
-                nc.sync.dma_start(out=down_words[:, g, :], in_=words_by_partition(down_w_words)[:, g, :])
+            load_words(1, gate_loaded, gate_w_words)
+            load_words(1, up_loaded, up_w_words)
+            load_planes(gate_w_scales, GATE_PLANES, slice(1024, 2048))
+            load_words(2, gate_loaded, gate_w_words)
+            load_planes(up_w_scales, UP_PLANES, slice(1024, 2048))
+            load_words(2, up_loaded, up_w_words)
+            load_words(3, gate_loaded, gate_w_words)
+            load_planes(gate_w_scales, GATE_PLANES, slice(2048, 3072))
+            load_words(3, up_loaded, up_w_words)
+            load_planes(up_w_scales, UP_PLANES, slice(2048, 3072))
+            load_words(4, gate_loaded, gate_w_words)
+            load_words(4, up_loaded, up_w_words)
+            load_words(5, gate_loaded, gate_w_words)
+            load_words(5, up_loaded, up_w_words)
+            load_down_planes(0)
+            load_down_words(0)
+            load_down_planes(1)
+            load_down_words(1)
+            load_down_words(2)
+            load_down_words(3)
+            load_down_words(4)
+            load_down_words(5)
             nc.sync.dma_start(out=down_spread[:], in_=down_s.partition_broadcast(P))
 
         x_grouped = keep.tile([P, X_PASSES, PACK * TOKENS], BF16, name="x_grouped", align_bytes=64)
@@ -215,10 +236,11 @@ def tile_cudaternaryexpertmodule_kernel(
         widen_vector(1)
         sort_jobs = []
         for c in range(1, BLOCKS):
-            sort_jobs.append((c, None, None, None))
             for loaded, in_order in ((gate_loaded, gate_sorted), (up_loaded, up_sorted)):
                 for g in range(X_PASSES):
                     sort_jobs.append((c, loaded, in_order, g))
+                if loaded is gate_loaded:
+                    sort_jobs.append((c, None, None, None))
 
         def run_sort_job(job):
             c, loaded, in_order, g = job
@@ -273,7 +295,7 @@ def tile_cudaternaryexpertmodule_kernel(
                 col = PACK * c + t
                 if t == 0 and c >= 2:
                     quantise_hidden(c - 2)
-                jobs_wanted = min(len(sort_jobs), (3 * (col + 1) + 1) // 2 + 1)
+                jobs_wanted = min(len(sort_jobs), 3 + col + col // 3)
                 for job in sort_jobs[jobs_done:jobs_wanted]:
                     run_sort_job(job)
                 jobs_done = jobs_wanted
@@ -309,7 +331,7 @@ def tile_cudaternaryexpertmodule_kernel(
             cols = slice(N_PASS * half + width * part, N_PASS * half + width * (part + 1))
             result = work.tile([P, width], F32, tag="result", bufs=OUT_BANKS + LAST_PARTS - 1)
             nc.vector.tensor_tensor(out=result[:], in0=acc[:], in1=down_spread[:, cols], op=MULT)
-            nc.sync.dma_start(out=out_rows[P * i : P * (i + 1), cols], in_=result[:])
+            nc.sync.dma_start(out=out_rows.rearrange("(p i) n -> p i n", i=TOKEN_TILES)[:, i, cols], in_=result[:])
 
         quantise_hidden(BLOCKS - 2)
         for i in range(TOKEN_TILES):

@@ -30,8 +30,8 @@ OUT_BANKS = TOKEN_TILES * OUT_HALVES
 FIRST_WAVE = 6
 LAST_PARTS = 2
 PLANES_FIRST = 2
-WARM_BEFORE_X = 6
-WARM_AFTER_X = 5
+WARM_BEFORE_X = 4
+WARM_BETWEEN = (1, 1, 1, 2)
 
 GATE_PLANES = 0
 UP_PLANES = 8
@@ -70,11 +70,13 @@ def tile_cudaternaryexpertmodule_kernel(
         ctx.enter_context(tc.manual_schedule())
 
         loaded_planes = keep.tile([P, INNER], U8, name="loaded_planes", align_bytes=64)
-        nc.vector.memset(loaded_planes[:].bitcast(I32), 0)
+        first_planes = loaded_planes[:, 0 : PLANES_FIRST * K_PASS]
+        nc.vector.memset(first_planes.bitcast(I32), 0)
+        zeros = keep.tile([P, N_PASS], BF16, name="zeros")
+        nc.vector.memset(zeros[:].bitcast(I32), 0)
+        nc.vector.memset(loaded_planes[:, PLANES_FIRST * K_PASS : INNER].bitcast(I32), 0)
         down_planes = keep.tile([P, 2, HIDDEN], U8, name="down_planes", align_bytes=64)
         nc.vector.memset(down_planes[:].rearrange("p b n -> p (b n)").bitcast(I32), 0)
-        zeros = keep.tile([P, N_PASS], BF16, name="zeros")
-        nc.gpsimd.memset(zeros[:], 0.0)
         ident_f32 = keep.tile([P, P], F32, name="ident_f32")
         make_identity(nc, ident_f32[:])
 
@@ -116,7 +118,7 @@ def tile_cudaternaryexpertmodule_kernel(
 
         vector_cols_bf16 = keep.tile([P, 2, VECTOR_PAD], BF16, name="vector_cols_bf16")
         for j, vector in enumerate((gate_s, up_s)):
-            nc.gpsimd.dma_start(
+            nc.sync.dma_start(
                 out=vector_cols_bf16[:, j, 0 : PACK * BLOCKS].rearrange("p (c t) -> p c t", t=PACK),
                 in_=vector.rearrange("(c p t) -> p c t", p=P, t=PACK),
             )
@@ -221,16 +223,17 @@ def tile_cudaternaryexpertmodule_kernel(
         for pair in range(TOKEN_TILES // 2):
             for g in range(X_PASSES):
                 turn_x(pair, g, nc.scalar.copy)
-        keep_warm(WARM_AFTER_X)
+                keep_warm(WARM_BETWEEN[X_PASSES * pair + g])
         quantise_x(0, 0)
-        quantise_x(0, 1)
         sort_planes(0, gate_planes)
         load_the_rest()
+        quantise_x(0, 1)
         quantise_x(1, 0)
+        sort_words(0, gate_loaded, gate_sorted, 0)
         quantise_x(1, 1)
-        for loaded, in_order in ((gate_loaded, gate_sorted), (up_loaded, up_sorted)):
-            for g in range(X_PASSES):
-                sort_words(0, loaded, in_order, g)
+        sort_words(0, gate_loaded, gate_sorted, 1)
+        sort_words(0, up_loaded, up_sorted, 0)
+        sort_words(0, up_loaded, up_sorted, 1)
         sort_planes(0, up_planes)
         widen_vector(0)
         widen_vector(1)
@@ -255,22 +258,22 @@ def tile_cudaternaryexpertmodule_kernel(
         h_codes = keep.tile([P, BLOCKS, TOKENS], U32, name="h_codes", align_bytes=64)
         h_scales = keep.tile([P, BLOCKS, TOKENS], U8, name="h_scales", align_bytes=64)
 
-        def multiply(c, t, words, planes, first_row):
-            acc = psum.tile([P, TOKENS], F32, tag="bank", name="acc")
+        def multiply(c, quarters, words, planes, first_row):
+            accs = [psum.tile([P, TOKENS], F32, tag="bank", name="acc") for t in quarters]
             for g in range(X_PASSES):
-                nc.tensor.matmul_mx(
-                    out=acc[:],
-                    lhsT=words[c][:, g, t, :].bitcast(FP8X4),
-                    lhsT_scale=planes[c][first_row + 4 * g : P, P * t : P * (t + 1)],
-                    rhs=x_codes[:, g, :].bitcast(FP8X4),
-                    rhs_scale=x_scales[:, g, :],
-                    start=(g == 0),
-                    stop=(g == X_PASSES - 1),
-                )
-            return acc
+                for acc, t in zip(accs, quarters):
+                    nc.tensor.matmul_mx(
+                        out=acc[:],
+                        lhsT=words[c][:, g, t, :].bitcast(FP8X4),
+                        lhsT_scale=planes[c][first_row + 4 * g : P, P * t : P * (t + 1)],
+                        rhs=x_codes[:, g, :].bitcast(FP8X4),
+                        rhs_scale=x_scales[:, g, :],
+                        start=(g == 0),
+                        stop=(g == X_PASSES - 1),
+                    )
+            return accs
 
-        def silu_of_gate(c, t):
-            gate_ps = multiply(c, t, gate_sorted, gate_planes, GATE_PLANES)
+        def silu_of_gate(c, t, gate_ps):
             gate = work.tile([P, TOKENS], F32, tag="gate", bufs=4)
             col = PACK * c + t
             nc.scalar.activation(out=gate[:], in_=gate_ps[:], func=SILU, scale=vector_cols[:, 0, col : col + 1])
@@ -288,10 +291,15 @@ def tile_cudaternaryexpertmodule_kernel(
         hiddens = []
         for c in range(BLOCKS):
             hiddens.append(work.tile([P, PACK, TOKENS], BF16, tag="hidden", name="hidden"))
-            first_gates = [silu_of_gate(c, t) for t in range(PACK)] if c == 0 else None
+            if c == 0:
+                gates_ps = multiply(c, range(PACK), gate_sorted, gate_planes, GATE_PLANES)
+                first_gates = [silu_of_gate(c, t, gates_ps[t]) for t in range(PACK)]
             for t in range(PACK):
-                gate = first_gates[t] if c == 0 else silu_of_gate(c, t)
-                up_ps = multiply(c, t, up_sorted, up_planes, UP_PLANES)
+                if c == 0:
+                    gate = first_gates[t]
+                else:
+                    gate = silu_of_gate(c, t, multiply(c, [t], gate_sorted, gate_planes, GATE_PLANES)[0])
+                up_ps = multiply(c, [t], up_sorted, up_planes, UP_PLANES)[0]
                 col = PACK * c + t
                 if t == 0 and c >= 2:
                     quantise_hidden(c - 2)

@@ -31,7 +31,7 @@ FIRST_WAVE = 6
 LAST_PARTS = 2
 PLANES_FIRST = 2
 WARM_BEFORE_X = 4
-WARM_BETWEEN = (1, 1, 1, 2)
+WARM_BETWEEN = (1, 1, 1, 1)
 
 GATE_PLANES = 0
 UP_PLANES = 8
@@ -75,7 +75,7 @@ def tile_cudaternaryexpertmodule_kernel(
         zeros = keep.tile([P, N_PASS], BF16, name="zeros")
         nc.vector.memset(zeros[:].bitcast(I32), 0)
         nc.vector.memset(loaded_planes[:, PLANES_FIRST * K_PASS : INNER].bitcast(I32), 0)
-        down_planes = keep.tile([P, 2, HIDDEN], U8, name="down_planes", align_bytes=64)
+        down_planes = keep.tile([P, 2, HIDDEN], U8, name="down_planes", align_bytes=256)
         nc.vector.memset(down_planes[:].rearrange("p b n -> p (b n)").bitcast(I32), 0)
         ident_f32 = keep.tile([P, P], F32, name="ident_f32")
         make_identity(nc, ident_f32[:])
@@ -130,7 +130,7 @@ def tile_cudaternaryexpertmodule_kernel(
         table_warmer = keep.tile([P, 1], F32, name="table_warmer")
         nc.scalar.activation(out=table_warmer[:], in_=ident_f32[:, 0:1], func=SILU)
 
-        down_words = keep.tile([P, BLOCKS, HIDDEN], I32, name="down_words", align_bytes=64)
+        down_words = keep.tile([P, BLOCKS, HIDDEN], I32, name="down_words", align_bytes=256)
         down_spread = keep.tile([P, HIDDEN], BF16, name="down_spread")
 
         def load_down_planes(group):
@@ -172,8 +172,8 @@ def tile_cudaternaryexpertmodule_kernel(
             nc.sync.dma_start(out=down_spread[:], in_=down_s.partition_broadcast(P))
 
         x_grouped = keep.tile([P, X_PASSES, PACK * TOKENS], BF16, name="x_grouped", align_bytes=64)
-        x_codes = keep.tile([P, X_PASSES, TOKENS], U32, name="x_codes", align_bytes=64)
-        x_scales = keep.tile([P, X_PASSES, TOKENS], U8, name="x_scales", align_bytes=64)
+        x_codes = keep.tile([P, X_PASSES, TOKENS], U32, name="x_codes", align_bytes=256)
+        x_scales = keep.tile([P, X_PASSES, TOKENS], U8, name="x_scales", align_bytes=256)
 
         def turn_x(pair, g, copy_out):
             turned = psum.tile([P, 2, 2 * P], F32, tag="bank", name="turned")
@@ -198,13 +198,13 @@ def tile_cudaternaryexpertmodule_kernel(
                 in_=x_grouped[:, g, PACK * 2 * P * pair : PACK * 2 * P * (pair + 1)],
             )
 
-        gate_planes = [keep.tile([P, K_PASS], U8, name="gate_planes%d" % c, align_bytes=64) for c in range(BLOCKS)]
-        up_planes = [keep.tile([P, K_PASS], U8, name="up_planes0", align_bytes=64)] + gate_planes[1:]
+        gate_planes = [keep.tile([P, K_PASS], U8, name="gate_planes%d" % c, align_bytes=256) for c in range(BLOCKS)]
+        up_planes = [keep.tile([P, K_PASS], U8, name="up_planes0", align_bytes=256)] + gate_planes[1:]
         gate_sorted = [
-            keep.tile([P, X_PASSES, PACK, P], I32, name="gate_sorted%d" % c, align_bytes=64) for c in range(BLOCKS)
+            keep.tile([P, X_PASSES, PACK, P], I32, name="gate_sorted%d" % c, align_bytes=256) for c in range(BLOCKS)
         ]
         up_sorted = [
-            keep.tile([P, X_PASSES, PACK, P], I32, name="up_sorted%d" % c, align_bytes=64) for c in range(BLOCKS)
+            keep.tile([P, X_PASSES, PACK, P], I32, name="up_sorted%d" % c, align_bytes=256) for c in range(BLOCKS)
         ]
 
         def sort_planes(c, planes):
@@ -220,16 +220,16 @@ def tile_cudaternaryexpertmodule_kernel(
                 in_=loaded[c][:, g, :].rearrange("p (m t) -> p m t", t=PACK),
             )
 
-        for pair in range(TOKEN_TILES // 2):
-            for g in range(X_PASSES):
+        for g in range(X_PASSES):
+            for pair in range(TOKEN_TILES // 2):
                 turn_x(pair, g, nc.scalar.copy)
-                keep_warm(WARM_BETWEEN[X_PASSES * pair + g])
+                keep_warm(WARM_BETWEEN[X_PASSES * g + pair])
         quantise_x(0, 0)
         sort_planes(0, gate_planes)
         load_the_rest()
-        quantise_x(0, 1)
         quantise_x(1, 0)
         sort_words(0, gate_loaded, gate_sorted, 0)
+        quantise_x(0, 1)
         quantise_x(1, 1)
         sort_words(0, gate_loaded, gate_sorted, 1)
         sort_words(0, up_loaded, up_sorted, 0)
@@ -255,8 +255,8 @@ def tile_cudaternaryexpertmodule_kernel(
         jobs_done = 0
 
         h_grouped = keep.tile([P, BLOCKS, PACK * TOKENS], BF16, name="h_grouped", align_bytes=64)
-        h_codes = keep.tile([P, BLOCKS, TOKENS], U32, name="h_codes", align_bytes=64)
-        h_scales = keep.tile([P, BLOCKS, TOKENS], U8, name="h_scales", align_bytes=64)
+        h_codes = keep.tile([P, BLOCKS, TOKENS], U32, name="h_codes", align_bytes=256)
+        h_scales = keep.tile([P, BLOCKS, TOKENS], U8, name="h_scales", align_bytes=256)
 
         def multiply(c, quarters, words, planes, first_row):
             accs = [psum.tile([P, TOKENS], F32, tag="bank", name="acc") for t in quarters]

from contextlib import ExitStack

import concourse.mybir as mybir
from concourse.masks import make_identity

BF16 = mybir.dt.bfloat16
F32 = mybir.dt.float32
I32 = mybir.dt.int32
U32 = mybir.dt.uint32
U8 = mybir.dt.uint8
FP8X4 = mybir.dt.float8_e4m3fn_x4
MULT = mybir.AluOpType.mult
SILU = mybir.ActivationFunctionType.Silu

P = 128
PACK = 4
K_PASS = P * PACK
N_PASS = 512

TOKENS = 512
HIDDEN = 1024
INNER = 3072
TOKEN_TILES = TOKENS // P
X_PASSES = HIDDEN // K_PASS
BLOCKS = INNER // K_PASS
OUT_HALVES = HIDDEN // N_PASS

BANKS = 8
OUT_BANKS = TOKEN_TILES * OUT_HALVES
FIRST_WAVE = 6
LAST_PARTS = 2
PLANES_FIRST = 2
WARM_BEFORE_X = 4
WARM_BETWEEN = (1, 1, 1, 1)

GATE_PLANES = 0
UP_PLANES = 8

VECTOR_PAD = 32

FLOPS = 2 * TOKENS * HIDDEN * INNER * 3


def words_by_partition(words):
    return words.rearrange("g p n t -> g p (n t)").bitcast(I32).rearrange("g p n -> p g n")


def tile_cudaternaryexpertmodule_kernel(
    tc,
    x,
    gate_w_words,
    gate_w_scales,
    up_w_words,
    up_w_scales,
    down_w_words,
    down_w_scales,
    gate_s,
    up_s,
    down_s,
    out,
):
    nc = tc.nc
    x_rows = x.flatten_outer_dims()
    out_rows = out.flatten_outer_dims()

    with ExitStack() as ctx:
        keep = ctx.enter_context(tc.tile_pool(name="keep", bufs=1))
        work = ctx.enter_context(tc.tile_pool(name="work", bufs=3))
        psum = ctx.enter_context(tc.psum_pool(name="psum", bufs=BANKS))
        ctx.enter_context(tc.manual_schedule())

        loaded_planes = keep.tile([P, INNER], U8, name="loaded_planes", align_bytes=64)
        first_planes = loaded_planes[:, 0 : PLANES_FIRST * K_PASS]
        nc.vector.memset(first_planes.bitcast(I32), 0)
        zeros = keep.tile([P, N_PASS], BF16, name="zeros")
        nc.vector.memset(zeros[:].bitcast(I32), 0)
        nc.vector.memset(loaded_planes[:, PLANES_FIRST * K_PASS : INNER].bitcast(I32), 0)
        down_planes = keep.tile([P, 2, HIDDEN], U8, name="down_planes", align_bytes=256)
        nc.vector.memset(down_planes[:].rearrange("p b n -> p (b n)").bitcast(I32), 0)
        ident_f32 = keep.tile([P, P], F32, name="ident_f32")
        make_identity(nc, ident_f32[:])

        def keep_warm(matmuls):
            unused = psum.tile([P, N_PASS], F32, tag="bank", name="unused")
            for n in range(matmuls):
                nc.tensor.matmul(out=unused[:], lhsT=zeros[:, 0:P], rhs=zeros[:], start=True, stop=True)

        keep_warm(WARM_BEFORE_X)

        x_sb = keep.tile([P, TOKEN_TILES, HIDDEN], BF16, name="x_sb")
        for pair in range(TOKEN_TILES // 2):
            tiles = slice(2 * pair, 2 * pair + 2)
            nc.sync.dma_start(
                out=x_sb[:, tiles, :].rearrange("p i k -> p (i k)"),
                in_=x_rows.rearrange("(p i) k -> p (i k)", i=TOKEN_TILES)[
                    :, 2 * HIDDEN * pair : 2 * HIDDEN * (pair + 1)
                ],
            )

        def load_planes(scales, first_row, cols):
            for quadrant in range(4):
                top = 32 * quadrant + first_row
                nc.sync.dma_start(
                    out=loaded_planes[top : top + 8, cols].bitcast(I32),
                    in_=scales[:, 4 * quadrant : 4 * quadrant + 4, cols].bitcast(I32),
                )

        gate_loaded = [keep.tile([P, X_PASSES, K_PASS], I32, name="gate_loaded%d" % c) for c in range(BLOCKS)]
        up_loaded = [keep.tile([P, X_PASSES, K_PASS], I32, name="up_loaded%d" % c) for c in range(BLOCKS)]

        def load_words(c, loaded, words):
            cols = slice(K_PASS * c, K_PASS * (c + 1))
            nc.sync.dma_start(out=loaded[c][:], in_=words_by_partition(words)[:, :, cols])

        load_planes(gate_w_scales, GATE_PLANES, slice(0, PLANES_FIRST * K_PASS))
        load_words(0, gate_loaded, gate_w_words)
        load_words(0, up_loaded, up_w_words)

        vector_cols_bf16 = keep.tile([P, 2, VECTOR_PAD], BF16, name="vector_cols_bf16")
        for j, vector in enumerate((gate_s, up_s)):
            nc.sync.dma_start(
                out=vector_cols_bf16[:, j, 0 : PACK * BLOCKS].rearrange("p (c t) -> p c t", t=PACK),
                in_=vector.rearrange("(c p t) -> p c t", p=P, t=PACK),
            )
        vector_cols = keep.tile([P, 2, PACK * BLOCKS], F32, name="vector_cols")

        def widen_vector(j):
            nc.vector.tensor_copy(out=vector_cols[:, j, :], in_=vector_cols_bf16[:, j, 0 : PACK * BLOCKS])

        table_warmer = keep.tile([P, 1], F32, name="table_warmer")
        nc.scalar.activation(out=table_warmer[:], in_=ident_f32[:, 0:1], func=SILU)

        down_words = keep.tile([P, BLOCKS, HIDDEN], I32, name="down_words", align_bytes=256)
        down_spread = keep.tile([P, HIDDEN], BF16, name="down_spread")

        def load_down_planes(group):
            passes = slice(4 * group, min(4 * group + 4, BLOCKS))
            for quadrant in range(4):
                top = 32 * quadrant
                nc.sync.dma_start(
                    out=down_planes[top : top + 4 * (passes.stop - passes.start), group, :].bitcast(I32),
                    in_=down_w_scales[passes, 4 * quadrant : 4 * quadrant + 4, :].bitcast(I32),
                )

        def load_down_words(g):
            nc.sync.dma_start(out=down_words[:, g, :], in_=words_by_partition(down_w_words)[:, g, :])

        def load_the_rest():
            load_planes(up_w_scales, UP_PLANES, slice(0, PLANES_FIRST * K_PASS))
            load_words(1, gate_loaded, gate_w_words)
            load_words(1, up_loaded, up_w_words)
            load_planes(gate_w_scales, GATE_PLANES, slice(1024, 2048))
            load_words(2, gate_loaded, gate_w_words)
            load_planes(up_w_scales, UP_PLANES, slice(1024, 2048))
            load_words(2, up_loaded, up_w_words)
            load_words(3, gate_loaded, gate_w_words)
            load_planes(gate_w_scales, GATE_PLANES, slice(2048, 3072))
            load_words(3, up_loaded, up_w_words)
            load_planes(up_w_scales, UP_PLANES, slice(2048, 3072))
            load_words(4, gate_loaded, gate_w_words)
            load_words(4, up_loaded, up_w_words)
            load_words(5, gate_loaded, gate_w_words)
            load_words(5, up_loaded, up_w_words)
            load_down_planes(0)
            load_down_words(0)
            load_down_planes(1)
            load_down_words(1)
            load_down_words(2)
            load_down_words(3)
            load_down_words(4)
            load_down_words(5)
            nc.sync.dma_start(out=down_spread[:], in_=down_s.partition_broadcast(P))

        x_grouped = keep.tile([P, X_PASSES, PACK * TOKENS], BF16, name="x_grouped", align_bytes=64)
        x_codes = keep.tile([P, X_PASSES, TOKENS], U32, name="x_codes", align_bytes=256)
        x_scales = keep.tile([P, X_PASSES, TOKENS], U8, name="x_scales", align_bytes=256)

        def turn_x(pair, g, copy_out):
            turned = psum.tile([P, 2, 2 * P], F32, tag="bank", name="turned")
            for half in range(2):
                words = x_sb[:, 2 * pair + half, K_PASS * g : K_PASS * (g + 1)].bitcast(F32)
                for u in range(2):
                    nc.tensor.transpose(
                        turned[:, u, P * half : P * (half + 1)], words[:, u : K_PASS // 2 : 2], ident_f32[:]
                    )
            copy_out(
                out=x_grouped[:, g, :].bitcast(F32)[:, 4 * P * pair : 4 * P * (pair + 1)].rearrange(
                    "p (w u) -> p w u", u=2
                ),
                in_=turned[:].rearrange("p u w -> p w u"),
            )

        def quantise_x(pair, g):
            tokens = slice(2 * P * pair, 2 * P * (pair + 1))
            nc.vector.quantize_mx(
                out=x_codes[:, g, tokens].bitcast(FP8X4),
                scales=x_scales[:, g, tokens],
                in_=x_grouped[:, g, PACK * 2 * P * pair : PACK * 2 * P * (pair + 1)],
            )

        gate_planes = [keep.tile([P, K_PASS], U8, name="gate_planes%d" % c, align_bytes=256) for c in range(BLOCKS)]
        up_planes = [keep.tile([P, K_PASS], U8, name="up_planes0", align_bytes=256)] + gate_planes[1:]
        gate_sorted = [
            keep.tile([P, X_PASSES, PACK, P], I32, name="gate_sorted%d" % c, align_bytes=256) for c in range(BLOCKS)
        ]
        up_sorted = [
            keep.tile([P, X_PASSES, PACK, P], I32, name="up_sorted%d" % c, align_bytes=256) for c in range(BLOCKS)
        ]

        def sort_planes(c, planes):
            cols = slice(K_PASS * c, K_PASS * (c + 1))
            nc.vector.tensor_copy(
                out=planes[c][:].rearrange("p (t m) -> p m t", t=PACK),
                in_=loaded_planes[:, cols].rearrange("p (m t) -> p m t", t=PACK),
            )

        def sort_words(c, loaded, in_order, g):
            nc.vector.tensor_copy(
                out=in_order[c][:, g, :, :].rearrange("p t m -> p m t"),
                in_=loaded[c][:, g, :].rearrange("p (m t) -> p m t", t=PACK),
            )

        for g in range(X_PASSES):
            for pair in range(TOKEN_TILES // 2):
                turn_x(pair, g, nc.scalar.copy)
                keep_warm(WARM_BETWEEN[X_PASSES * g + pair])
        quantise_x(0, 0)
        sort_planes(0, gate_planes)
        load_the_rest()
        quantise_x(1, 0)
        sort_words(0, gate_loaded, gate_sorted, 0)
        quantise_x(0, 1)
        quantise_x(1, 1)
        sort_words(0, gate_loaded, gate_sorted, 1)
        sort_words(0, up_loaded, up_sorted, 0)
        sort_words(0, up_loaded, up_sorted, 1)
        sort_planes(0, up_planes)
        widen_vector(0)
        widen_vector(1)
        sort_jobs = []
        for c in range(1, BLOCKS):
            for loaded, in_order in ((gate_loaded, gate_sorted), (up_loaded, up_sorted)):
                for g in range(X_PASSES):
                    sort_jobs.append((c, loaded, in_order, g))
                if loaded is gate_loaded:
                    sort_jobs.append((c, None, None, None))

        def run_sort_job(job):
            c, loaded, in_order, g = job
            if loaded is None:
                sort_planes(c, gate_planes)
            else:
                sort_words(c, loaded, in_order, g)

        jobs_done = 0

        h_grouped = keep.tile([P, BLOCKS, PACK * TOKENS], BF16, name="h_grouped", align_bytes=64)
        h_codes = keep.tile([P, BLOCKS, TOKENS], U32, name="h_codes", align_bytes=256)
        h_scales = keep.tile([P, BLOCKS, TOKENS], U8, name="h_scales", align_bytes=256)

        def multiply(c, quarters, words, planes, first_row):
            accs = [psum.tile([P, TOKENS], F32, tag="bank", name="acc") for t in quarters]
            for g in range(X_PASSES):
                for acc, t in zip(accs, quarters):
                    nc.tensor.matmul_mx(
                        out=acc[:],
                        lhsT=words[c][:, g, t, :].bitcast(FP8X4),
                        lhsT_scale=planes[c][first_row + 4 * g : P, P * t : P * (t + 1)],
                        rhs=x_codes[:, g, :].bitcast(FP8X4),
                        rhs_scale=x_scales[:, g, :],
                        start=(g == 0),
                        stop=(g == X_PASSES - 1),
                    )
            return accs

        def silu_of_gate(c, t, gate_ps):
            gate = work.tile([P, TOKENS], F32, tag="gate", bufs=4)
            col = PACK * c + t
            nc.scalar.activation(out=gate[:], in_=gate_ps[:], func=SILU, scale=vector_cols[:, 0, col : col + 1])
            return gate

        def group_hidden(c, hidden, i, copy):
            copy(
                out=h_grouped[:, c, PACK * P * i : PACK * P * (i + 1)].rearrange("p (n t) -> p n t", t=PACK),
                in_=hidden[:, :, P * i : P * (i + 1)].rearrange("p t n -> p n t"),
            )

        def quantise_hidden(c):
            nc.vector.quantize_mx(out=h_codes[:, c, :].bitcast(FP8X4), scales=h_scales[:, c, :], in_=h_grouped[:, c, :])

        hiddens = []
        for c in range(BLOCKS):
            hiddens.append(work.tile([P, PACK, TOKENS], BF16, tag="hidden", name="hidden"))
            if c == 0:
                gates_ps = multiply(c, range(PACK), gate_sorted, gate_planes, GATE_PLANES)
                first_gates = [silu_of_gate(c, t, gates_ps[t]) for t in range(PACK)]
            for t in range(PACK):
                if c == 0:
                    gate = first_gates[t]
                else:
                    gate = silu_of_gate(c, t, multiply(c, [t], gate_sorted, gate_planes, GATE_PLANES)[0])
                up_ps = multiply(c, [t], up_sorted, up_planes, UP_PLANES)[0]
                col = PACK * c + t
                if t == 0 and c >= 2:
                    quantise_hidden(c - 2)
                jobs_wanted = min(len(sort_jobs), 3 + col + col // 3)
                for job in sort_jobs[jobs_done:jobs_wanted]:
                    run_sort_job(job)
                jobs_done = jobs_wanted
                nc.vector.scalar_tensor_tensor(
                    out=hiddens[c][:, t, :],
                    in0=up_ps[:],
                    scalar=vector_cols[:, 1, col : col + 1],
                    in1=gate[:],
                    op0=MULT,
                    op1=MULT,
                )
                if c >= 1:
                    group_hidden(c - 1, hiddens[c - 1], t, nc.scalar.copy)

        def down_pass(acc, a, g, part=0, parts=1):
            i, half = divmod(a, OUT_HALVES)
            tokens = slice(P * i, P * (i + 1))
            width = N_PASS // parts
            cols = slice(N_PASS * half + width * part, N_PASS * half + width * (part + 1))
            nc.tensor.matmul_mx(
                out=acc[:],
                lhsT=h_codes[:, g, tokens].bitcast(FP8X4),
                lhsT_scale=h_scales[:, g, tokens],
                rhs=down_words[:, g, cols].bitcast(FP8X4),
                rhs_scale=down_planes[4 * (g % 4) : P, g // 4, cols],
                start=(g == 0),
                stop=(g == BLOCKS - 1),
            )

        def finish(acc, a, part=0, parts=1):
            i, half = divmod(a, OUT_HALVES)
            width = N_PASS // parts
            cols = slice(N_PASS * half + width * part, N_PASS * half + width * (part + 1))
            result = work.tile([P, width], F32, tag="result", bufs=OUT_BANKS + LAST_PARTS - 1)
            nc.vector.tensor_tensor(out=result[:], in0=acc[:], in1=down_spread[:, cols], op=MULT)
            nc.sync.dma_start(out=out_rows.rearrange("(p i) n -> p i n", i=TOKEN_TILES)[:, i, cols], in_=result[:])

        quantise_hidden(BLOCKS - 2)
        for i in range(TOKEN_TILES):
            group_hidden(BLOCKS - 1, hiddens[BLOCKS - 1], i, nc.scalar.copy if i < 2 else nc.vector.tensor_copy)
        accs = []
        for a in range(FIRST_WAVE):
            accs.append(psum.tile([P, N_PASS], F32, tag="bank", name="out_ps"))
            for g in range(BLOCKS - 2):
                down_pass(accs[a], a, g)
        for a in range(FIRST_WAVE):
            down_pass(accs[a], a, BLOCKS - 2)
        quantise_hidden(BLOCKS - 1)
        for a in range(FIRST_WAVE):
            down_pass(accs[a], a, BLOCKS - 1)
            finish(accs[a], a)
        for a in range(FIRST_WAVE, OUT_BANKS - 1):
            late_ps = psum.tile([P, N_PASS], F32, tag="bank", name="late_ps")
            for g in range(BLOCKS):
                down_pass(late_ps, a, g)
            finish(late_ps, a)
        for part in range(LAST_PARTS):
            part_ps = psum.tile([P, N_PASS // LAST_PARTS], F32, tag="bank", name="part_ps")
            for g in range(BLOCKS):
                down_pass(part_ps, OUT_BANKS - 1, g, part, LAST_PARTS)
            finish(part_ps, OUT_BANKS - 1, part, LAST_PARTS)
